import numpy as np
import ml_dtypes


def mxq(x, axis, fmt="e4m3"):
    dtype, down = {"e4m3": (ml_dtypes.float8_e4m3fn, 7), "e5m2": (ml_dtypes.float8_e5m2, 14)}[fmt]
    v = np.moveaxis(np.asarray(x, np.float32).astype(ml_dtypes.bfloat16).astype(np.float64), axis, -1)
    blocks = v.reshape(v.shape[:-1] + (-1, 32))
    amax = np.abs(blocks).max(-1, keepdims=True)
    byte = np.maximum(np.where(amax > 0, np.frexp(amax)[1] - 1 + 127, 0) - down, 1)
    scale = np.exp2(byte - 127.0)
    codes = (blocks / scale).astype(np.float32).astype(dtype).astype(np.float64)
    return np.moveaxis((codes * scale).reshape(v.shape), -1, axis)


WIDE = False


def mx_kscale(k):
    if not WIDE:
        return np.ones(k)
    levels = np.array([20, -20, 10, -10, 0])
    a = np.random.permutation(np.resize(levels, k // 512 * 4)).reshape(k // 512, 4)
    idx = np.arange(k)
    return np.exp2(a[idx // 512, idx % 128 // 32])


BF16 = ml_dtypes.bfloat16


def bf(x):
    return np.asarray(x, np.float32).astype(BF16)


def f64(x):
    return np.asarray(x).astype(np.float64)


B, N, SIZE, CH = 1024, 16, 1024, 512


def sigmoid(v):
    return 1.0 / (1.0 + np.exp(-v))


def gates(z0, h_tilde, W_i, U_i, b_i, W_o, U_o, b_o, W_u, U_u, b_u):
    z = f64(z0)
    ht = f64(h_tilde)
    i = sigmoid(z @ f64(W_i).T + ht @ f64(U_i).T + f64(b_i))
    o = sigmoid(z @ f64(W_o).T + ht @ f64(U_o).T + f64(b_o))
    u = np.tanh(z @ f64(W_u).T + ht @ f64(U_u).T + f64(b_u))
    return i, o, u


def setup_inputs():
    s = mx_kscale(CH)
    d = {"z0": bf(np.random.standard_normal((B, SIZE))),
         "h_tilde": bf(np.random.standard_normal((B, CH)) * np.sqrt(N)),
         "fc_sum": bf(np.random.standard_normal((B, CH)) * 1.2)}
    for g in ("i", "o", "u"):
        d["W_" + g] = bf(np.random.standard_normal((CH, SIZE)) / np.sqrt(SIZE) / s[:, None])
        d["U_" + g] = bf(np.random.standard_normal((CH, CH)) / np.sqrt(CH * N))
        d["b_" + g] = bf(np.random.standard_normal(CH) * 0.5)
    go = np.random.standard_normal((B, 2 * CH)) * np.exp2(np.random.randint(-12, 1, (B, 1))) * 64.0 * np.concatenate([s, s])
    i, o, u = gates(d["z0"], d["h_tilde"], f64(d["W_i"]) * s[:, None], d["U_i"], d["b_i"], f64(d["W_o"]) * s[:, None], d["U_o"], d["b_o"], f64(d["W_u"]) * s[:, None], d["U_u"], d["b_u"])
    d["i_j"] = np.asarray(i, np.float32)
    d["o_j"] = np.asarray(o, np.float32)
    d["u_j"] = np.asarray(u, np.float32)
    d["grad_out"] = bf(go)
    return d


def reference(z0, h_tilde, fc_sum, W_i, U_i, b_i, W_o, U_o, b_o, W_u, U_u, b_u, i_j, o_j, u_j, grad_out):
    i = f64(i_j)
    o = f64(o_j)
    u = f64(u_j)
    g = f64(grad_out)
    gh = g[:, :CH]
    gc = g[:, CH:]
    tc = np.tanh(i * u + f64(fc_sum))
    dc = gc + gh * o * (1.0 - tc * tc)
    da_i = dc * u * i * (1.0 - i)
    da_o = gh * tc * o * (1.0 - o)
    da_u = dc * i * (1.0 - u * u)
    p_i = mxq(da_i, 1, "e5m2") @ mxq(f64(W_i), 0, "e4m3")
    p_o = mxq(da_o, 1, "e5m2") @ mxq(f64(W_o), 0, "e4m3")
    p_u = mxq(da_u, 1, "e5m2") @ mxq(f64(W_u), 0, "e4m3")
    return p_i + p_o + p_u

@@ -1,0 +1,206 @@
+import concourse.mybir as mybir
+from concourse.masks import make_identity
+
+F32 = mybir.dt.float32
+BF16 = mybir.dt.bfloat16
+U32 = mybir.dt.uint32
+U8 = mybir.dt.uint8
+E4M3_X4 = mybir.dt.float8_e4m3fn_x4
+E5M2_X4 = mybir.dt.float8_e5m2_x4
+ALU = mybir.AluOpType
+ACT = mybir.ActivationFunctionType
+
+P = 128
+PACK = 4
+NODES = 1024
+CH = 512
+SIZE = 1024
+N_TILE = 512
+NODE_TILES = NODES // P
+HALVES = SIZE // N_TILE
+GATES = 3
+GATE_I, GATE_O, GATE_U = 0, 1, 2
+
+FLOPS = 2 * NODES * SIZE * CH * GATES
+BYTES = NODES * CH * (2 + 3 * 4) + NODES * 2 * CH * 2 + GATES * CH * SIZE * 2 + NODES * SIZE * 4
+
+FIRST_MULTIPLY_STEP = GATES + 2
+
+
+def tile_treelstm_pb_v_kernel(
+    tc, z0, h_tilde, fc_sum, W_i, U_i, b_i, W_o, U_o, b_o, W_u, U_u, b_u, i_j, o_j, u_j, grad_out, out
+):
+    nc = tc.nc
+    weights = (W_i, W_o, W_u)
+
+    with tc.tile_pool(name="const", bufs=1) as const, tc.tile_pool(name="inputs", bufs=NODE_TILES) as inputs, tc.tile_pool(
+        name="wraw", bufs=GATES
+    ) as wraw, tc.tile_pool(name="wgrp", bufs=2 * HALVES) as wgrp, tc.tile_pool(name="work", bufs=2) as work, tc.tile_pool(
+        name="grouped", bufs=2 * GATES
+    ) as grouped, tc.tile_pool(name="codes", bufs=NODE_TILES) as codes, tc.tile_pool(name="results", bufs=4) as results, tc.psum_pool(
+        name="psum_t", bufs=4
+    ) as psum_t, tc.psum_pool(name="psum_o", bufs=4) as psum_o, tc.manual_schedule():
+        ident = const.tile([P, P], BF16)
+        make_identity(nc, ident[:])
+        w_codes = const.tile([P, GATES, SIZE], U32, align_bytes=64)
+        w_scales = const.tile([P, GATES, SIZE], U8, align_bytes=64)
+
+        loaded = {}
+        w_raw = {}
+        w_grouped = {}
+        kept = {}
+        turned = {}
+        da_grouped = {}
+        da_packed = {}
+
+        def load_nodes(n):
+            rows = slice(n * P, (n + 1) * P)
+            i_sb = inputs.tile([P, CH], F32)
+            u_sb = inputs.tile([P, CH], F32)
+            fc_sb = inputs.tile([P, CH], BF16)
+            o_sb = inputs.tile([P, CH], F32)
+            g_sb = inputs.tile([P, 2 * CH], BF16)
+            nc.sync.dma_start(out=i_sb[:], in_=i_j[rows, :])
+            nc.sync.dma_start(out=u_sb[:], in_=u_j[rows, :])
+            nc.sync.dma_start(out=fc_sb[:], in_=fc_sum[rows, :])
+            nc.sync.dma_start(out=o_sb[:], in_=o_j[rows, :])
+            nc.sync.dma_start(out=g_sb[:], in_=grad_out[rows, :])
+            loaded[n] = (i_sb, o_sb, u_sb, fc_sb, g_sb)
+
+        def load_weight(g):
+            raw = wraw.tile([P, PACK, SIZE], BF16)
+            nc.sync.dma_start(out=raw[:], in_=weights[g].rearrange("(t p) n -> p t n", p=P))
+            w_raw[g] = raw
+
+        def regroup_weight(g):
+            for h in range(HALVES):
+                cols = slice(h * N_TILE, (h + 1) * N_TILE)
+                w_grp = wgrp.tile([P, N_TILE, PACK], BF16, align_bytes=64)
+                nc.scalar.copy(
+                    out=w_grp[:].rearrange("p (c i) t -> p c t i", i=4),
+                    in_=w_raw[g][:, :, cols].rearrange("p t (c i) -> p c t i", i=4),
+                )
+                w_grouped[(g, h)] = w_grp
+
+        def quantise_weight(g):
+            for h in range(HALVES):
+                cols = slice(h * N_TILE, (h + 1) * N_TILE)
+                nc.vector.quantize_mx(
+                    out=w_codes[:, g, cols].bitcast(E4M3_X4),
+                    scales=w_scales[:, g, cols],
+                    in_=w_grouped[(g, h)][:].rearrange("p n t -> p (n t)"),
+                )
+
+        def front(n):
+            i_sb, o_sb, u_sb, fc_sb, g_sb = loaded[n]
+            gh = g_sb[:, 0:CH]
+            u_sq = work.tile([P, CH], F32)
+            nc.scalar.activation(out=u_sq[:], in_=u_sb[:], func=ACT.Square)
+            iu = work.tile([P, CH], F32)
+            nc.vector.tensor_tensor(out=iu[:], in0=i_sb[:], in1=u_sb[:], op=ALU.mult)
+            cell = work.tile([P, CH], F32)
+            nc.vector.tensor_tensor(out=cell[:], in0=iu[:], in1=fc_sb[:], op=ALU.add)
+            gho = work.tile([P, CH], F32)
+            nc.vector.tensor_tensor(out=gho[:], in0=gh, in1=o_sb[:], op=ALU.mult)
+            neg_o = work.tile([P, CH], F32)
+            nc.vector.scalar_tensor_tensor(out=neg_o[:], in0=o_sb[:], scalar=1.0, in1=gho[:], op0=ALU.subtract, op1=ALU.mult)
+            neg_i = work.tile([P, CH], F32)
+            nc.vector.scalar_tensor_tensor(out=neg_i[:], in0=i_sb[:], scalar=1.0, in1=iu[:], op0=ALU.subtract, op1=ALU.mult)
+            neg_u = work.tile([P, CH], F32)
+            nc.vector.scalar_tensor_tensor(out=neg_u[:], in0=u_sq[:], scalar=1.0, in1=i_sb[:], op0=ALU.subtract, op1=ALU.mult)
+            kept[n] = (cell, gho, neg_o, neg_i, neg_u)
+
+        def tanh_of_cell(n):
+            cell, gho, neg_o, neg_i, neg_u = kept[n]
+            neg_tc = work.tile([P, CH], F32)
+            nc.scalar.activation(out=neg_tc[:], in_=cell[:], func=ACT.Tanh, scale=-1.0)
+            tc_sq = work.tile([P, CH], F32)
+            nc.scalar.activation(out=tc_sq[:], in_=neg_tc[:], func=ACT.Square)
+            kept[n] = (neg_tc, tc_sq, gho, neg_o, neg_i, neg_u)
+
+        def transpose(n, g, da):
+            da_t = psum_t.tile([P, PACK, P], BF16)
+            for t in range(PACK):
+                nc.tensor.transpose(da_t[:, t, :], da[:, g, t * P : (t + 1) * P], ident[:])
+            turned[(n, g)] = da_t
+
+        def back(n):
+            neg_tc, tc_sq, gho, neg_o, neg_i, neg_u = kept[n]
+            gc = loaded[n][4][:, CH : 2 * CH]
+            da = work.tile([P, GATES, CH], BF16)
+            nc.vector.tensor_tensor(out=da[:, GATE_O, :], in0=neg_o[:], in1=neg_tc[:], op=ALU.mult)
+            transpose(n, GATE_O, da)
+            neg_dc = work.tile([P, CH], F32)
+            nc.vector.scalar_tensor_tensor(out=neg_dc[:], in0=tc_sq[:], scalar=1.0, in1=gho[:], op0=ALU.subtract, op1=ALU.mult)
+            nc.vector.tensor_tensor(out=neg_dc[:], in0=neg_dc[:], in1=gc, op=ALU.subtract)
+            nc.vector.tensor_tensor(out=da[:, GATE_I, :], in0=neg_dc[:], in1=neg_i[:], op=ALU.mult)
+            transpose(n, GATE_I, da)
+            nc.vector.tensor_tensor(out=da[:, GATE_U, :], in0=neg_dc[:], in1=neg_u[:], op=ALU.mult)
+            transpose(n, GATE_U, da)
+
+        def regroup(n):
+            for g in (GATE_O, GATE_I, GATE_U):
+                da_grp = grouped.tile([P, P, PACK], BF16, align_bytes=64)
+                nc.scalar.copy(out=da_grp[:], in_=turned[(n, g)][:].rearrange("p t n -> p n t"))
+                da_grouped[(n, g)] = da_grp
+
+        def quantise(n):
+            da_codes = codes.tile([P, GATES, P], U32, align_bytes=64)
+            da_scales = codes.tile([P, GATES, P], U8, align_bytes=64)
+            for g in (GATE_O, GATE_I, GATE_U):
+                nc.vector.quantize_mx(
+                    out=da_codes[:, g, :].bitcast(E5M2_X4),
+                    scales=da_scales[:, g, :],
+                    in_=da_grouped[(n, g)][:].rearrange("p n t -> p (n t)"),
+                )
+            da_packed[n] = (da_codes, da_scales)
+
+        def multiply(n):
+            da_codes, da_scales = da_packed[n]
+            acc = [psum_o.tile([P, N_TILE], F32, name="acc") for h in range(HALVES)]
+            order = (GATE_O, GATE_I, GATE_U)
+            for g in order:
+                for h in range(HALVES):
+                    cols = slice(h * N_TILE, (h + 1) * N_TILE)
+                    nc.tensor.matmul_mx(
+                        out=acc[h][:],
+                        lhsT=da_codes[:, g, :].bitcast(E5M2_X4),
+                        lhsT_scale=da_scales[:, g, :],
+                        rhs=w_codes[:, g, cols].bitcast(E4M3_X4),
+                        rhs_scale=w_scales[:, g, cols],
+                        start=(g == order[0]),
+                        stop=(g == order[-1]),
+                    )
+            for h in range(HALVES):
+                result = results.tile([P, N_TILE], F32)
+                nc.scalar.copy(out=result[:], in_=acc[h][:])
+                nc.sync.dma_start(out=out[n * P : (n + 1) * P, h * N_TILE : (h + 1) * N_TILE], in_=result[:])
+
+        load_nodes(0)
+        load_nodes(1)
+        for g in range(GATES):
+            load_weight(g)
+            load_nodes(2 + g)
+        for n in range(2 + GATES, NODE_TILES):
+            load_nodes(n)
+
+        multiplied = 0
+        for s in range(NODE_TILES + 3):
+            if s < NODE_TILES:
+                front(s)
+            if 0 <= s - 2 < NODE_TILES:
+                regroup(s - 2)
+            if s >= FIRST_MULTIPLY_STEP:
+                for n in range(multiplied, s - 2):
+                    multiply(n)
+                multiplied = s - 2
+            if s < NODE_TILES:
+                tanh_of_cell(s)
+            if 0 <= s - 1 < NODE_TILES:
+                back(s - 1)
+            if 0 <= s - 2 < NODE_TILES:
+                quantise(s - 2)
+            if 0 <= s - 1 < GATES:
+                regroup_weight(s - 1)
+            if 0 <= s - 2 < GATES:
+                quantise_weight(s - 2)

@@ -25,6 +25,7 @@ FLOPS = 2 * NODES * SIZE * CH * GATES
 BYTES = NODES * CH * (2 + 3 * 4) + NODES * 2 * CH * 2 + GATES * CH * SIZE * 2 + NODES * SIZE * 4
 
 FIRST_MULTIPLY_STEP = GATES + 2
+MULTIPLIES_PER_STEP = 2
 
 
 def tile_treelstm_pb_v_kernel(
@@ -57,14 +58,14 @@ def tile_treelstm_pb_v_kernel(
             rows = slice(n * P, (n + 1) * P)
             i_sb = inputs.tile([P, CH], F32)
             u_sb = inputs.tile([P, CH], F32)
-            fc_sb = inputs.tile([P, CH], BF16)
-            o_sb = inputs.tile([P, CH], F32)
             g_sb = inputs.tile([P, 2 * CH], BF16)
+            o_sb = inputs.tile([P, CH], F32)
+            fc_sb = inputs.tile([P, CH], BF16)
             nc.sync.dma_start(out=i_sb[:], in_=i_j[rows, :])
             nc.sync.dma_start(out=u_sb[:], in_=u_j[rows, :])
-            nc.sync.dma_start(out=fc_sb[:], in_=fc_sum[rows, :])
-            nc.sync.dma_start(out=o_sb[:], in_=o_j[rows, :])
             nc.sync.dma_start(out=g_sb[:], in_=grad_out[rows, :])
+            nc.sync.dma_start(out=o_sb[:], in_=o_j[rows, :])
+            nc.sync.dma_start(out=fc_sb[:], in_=fc_sum[rows, :])
             loaded[n] = (i_sb, o_sb, u_sb, fc_sb, g_sb)
 
         def load_weight(g):
@@ -95,48 +96,78 @@ def tile_treelstm_pb_v_kernel(
             i_sb, o_sb, u_sb, fc_sb, g_sb = loaded[n]
             gh = g_sb[:, 0:CH]
             u_sq = work.tile([P, CH], F32)
-            nc.scalar.activation(out=u_sq[:], in_=u_sb[:], func=ACT.Square)
             iu = work.tile([P, CH], F32)
-            nc.vector.tensor_tensor(out=iu[:], in0=i_sb[:], in1=u_sb[:], op=ALU.mult)
             cell = work.tile([P, CH], F32)
-            nc.vector.tensor_tensor(out=cell[:], in0=iu[:], in1=fc_sb[:], op=ALU.add)
-            gho = work.tile([P, CH], F32)
-            nc.vector.tensor_tensor(out=gho[:], in0=gh, in1=o_sb[:], op=ALU.mult)
-            neg_o = work.tile([P, CH], F32)
-            nc.vector.scalar_tensor_tensor(out=neg_o[:], in0=o_sb[:], scalar=1.0, in1=gho[:], op0=ALU.subtract, op1=ALU.mult)
-            neg_i = work.tile([P, CH], F32)
-            nc.vector.scalar_tensor_tensor(out=neg_i[:], in0=i_sb[:], scalar=1.0, in1=iu[:], op0=ALU.subtract, op1=ALU.mult)
-            neg_u = work.tile([P, CH], F32)
-            nc.vector.scalar_tensor_tensor(out=neg_u[:], in0=u_sq[:], scalar=1.0, in1=i_sb[:], op0=ALU.subtract, op1=ALU.mult)
-            kept[n] = (cell, gho, neg_o, neg_i, neg_u)
-
-        def tanh_of_cell(n):
-            cell, gho, neg_o, neg_i, neg_u = kept[n]
             neg_tc = work.tile([P, CH], F32)
-            nc.scalar.activation(out=neg_tc[:], in_=cell[:], func=ACT.Tanh, scale=-1.0)
             tc_sq = work.tile([P, CH], F32)
-            nc.scalar.activation(out=tc_sq[:], in_=neg_tc[:], func=ACT.Square)
+            gho = work.tile([P, CH], F32)
+            neg_o = work.tile([P, CH], F32)
+            neg_i = work.tile([P, CH], F32)
+            neg_u = work.tile([P, CH], F32)
             kept[n] = (neg_tc, tc_sq, gho, neg_o, neg_i, neg_u)
+            nc.scalar.activation(out=u_sq[:], in_=u_sb[:], func=ACT.Square)
 
-        def transpose(n, g, da):
-            da_t = psum_t.tile([P, PACK, P], BF16)
-            for t in range(PACK):
-                nc.tensor.transpose(da_t[:, t, :], da[:, g, t * P : (t + 1) * P], ident[:])
-            turned[(n, g)] = da_t
+            def make_iu():
+                nc.vector.tensor_tensor(out=iu[:], in0=i_sb[:], in1=u_sb[:], op=ALU.mult)
+
+            def make_gho():
+                nc.vector.tensor_tensor(out=gho[:], in0=gh, in1=o_sb[:], op=ALU.mult)
+
+            def make_tanh():
+                nc.vector.tensor_tensor(out=cell[:], in0=iu[:], in1=fc_sb[:], op=ALU.add)
+                nc.scalar.activation(out=neg_tc[:], in_=cell[:], func=ACT.Tanh, scale=-1.0)
+                nc.scalar.activation(out=tc_sq[:], in_=neg_tc[:], func=ACT.Square)
+
+            def make_neg_o():
+                nc.vector.scalar_tensor_tensor(
+                    out=neg_o[:], in0=o_sb[:], scalar=1.0, in1=gho[:], op0=ALU.subtract, op1=ALU.mult
+                )
+
+            def make_neg_i():
+                nc.vector.scalar_tensor_tensor(
+                    out=neg_i[:], in0=i_sb[:], scalar=1.0, in1=iu[:], op0=ALU.subtract, op1=ALU.mult
+                )
+
+            def make_neg_u():
+                nc.vector.scalar_tensor_tensor(
+                    out=neg_u[:], in0=u_sq[:], scalar=1.0, in1=i_sb[:], op0=ALU.subtract, op1=ALU.mult
+                )
+
+            return [make_iu, make_gho, make_tanh, make_neg_o, make_neg_i, make_neg_u]
 
         def back(n):
             neg_tc, tc_sq, gho, neg_o, neg_i, neg_u = kept[n]
             gc = loaded[n][4][:, CH : 2 * CH]
             da = work.tile([P, GATES, CH], BF16)
-            nc.vector.tensor_tensor(out=da[:, GATE_O, :], in0=neg_o[:], in1=neg_tc[:], op=ALU.mult)
-            transpose(n, GATE_O, da)
             neg_dc = work.tile([P, CH], F32)
-            nc.vector.scalar_tensor_tensor(out=neg_dc[:], in0=tc_sq[:], scalar=1.0, in1=gho[:], op0=ALU.subtract, op1=ALU.mult)
-            nc.vector.tensor_tensor(out=neg_dc[:], in0=neg_dc[:], in1=gc, op=ALU.subtract)
-            nc.vector.tensor_tensor(out=da[:, GATE_I, :], in0=neg_dc[:], in1=neg_i[:], op=ALU.mult)
-            transpose(n, GATE_I, da)
-            nc.vector.tensor_tensor(out=da[:, GATE_U, :], in0=neg_dc[:], in1=neg_u[:], op=ALU.mult)
-            transpose(n, GATE_U, da)
+
+            def transpose(g):
+                da_t = psum_t.tile([P, PACK, P], BF16)
+                for t in range(PACK):
+                    nc.tensor.transpose(da_t[:, t, :], da[:, g, t * P : (t + 1) * P], ident[:])
+                turned[(n, g)] = da_t
+
+            def make_da_o():
+                nc.vector.tensor_tensor(out=da[:, GATE_O, :], in0=neg_o[:], in1=neg_tc[:], op=ALU.mult)
+                transpose(GATE_O)
+
+            def make_masked():
+                nc.vector.scalar_tensor_tensor(
+                    out=neg_dc[:], in0=tc_sq[:], scalar=1.0, in1=gho[:], op0=ALU.subtract, op1=ALU.mult
+                )
+
+            def make_neg_dc():
+                nc.vector.tensor_tensor(out=neg_dc[:], in0=neg_dc[:], in1=gc, op=ALU.subtract)
+
+            def make_da_i():
+                nc.vector.tensor_tensor(out=da[:, GATE_I, :], in0=neg_dc[:], in1=neg_i[:], op=ALU.mult)
+                transpose(GATE_I)
+
+            def make_da_u():
+                nc.vector.tensor_tensor(out=da[:, GATE_U, :], in0=neg_dc[:], in1=neg_u[:], op=ALU.mult)
+                transpose(GATE_U)
+
+            return [make_da_o, make_masked, make_neg_dc, make_da_i, make_da_u]
 
         def regroup(n):
             for g in (GATE_O, GATE_I, GATE_U):
@@ -158,8 +189,7 @@ def tile_treelstm_pb_v_kernel(
         def multiply(n):
             da_codes, da_scales = da_packed[n]
             acc = [psum_o.tile([P, N_TILE], F32, name="acc") for h in range(HALVES)]
-            order = (GATE_O, GATE_I, GATE_U)
-            for g in order:
+            for g in range(GATES):
                 for h in range(HALVES):
                     cols = slice(h * N_TILE, (h + 1) * N_TILE)
                     nc.tensor.matmul_mx(
@@ -168,8 +198,8 @@ def tile_treelstm_pb_v_kernel(
                         lhsT_scale=da_scales[:, g, :],
                         rhs=w_codes[:, g, cols].bitcast(E4M3_X4),
                         rhs_scale=w_scales[:, g, cols],
-                        start=(g == order[0]),
-                        stop=(g == order[-1]),
+                        start=(g == 0),
+                        stop=(g == GATES - 1),
                     )
             for h in range(HALVES):
                 result = results.tile([P, N_TILE], F32)
@@ -186,21 +216,23 @@ def tile_treelstm_pb_v_kernel(
 
         multiplied = 0
         for s in range(NODE_TILES + 3):
-            if s < NODE_TILES:
-                front(s)
+            front_steps = front(s) if s < NODE_TILES else []
+            back_steps = back(s - 1) if 0 <= s - 1 < NODE_TILES else []
             if 0 <= s - 2 < NODE_TILES:
                 regroup(s - 2)
             if s >= FIRST_MULTIPLY_STEP:
-                for n in range(multiplied, s - 2):
+                upto = min(s - 2, multiplied + MULTIPLIES_PER_STEP)
+                for n in range(multiplied, upto):
                     multiply(n)
-                multiplied = s - 2
-            if s < NODE_TILES:
-                tanh_of_cell(s)
-            if 0 <= s - 1 < NODE_TILES:
-                back(s - 1)
+                multiplied = upto
+            for k in range(max(len(front_steps), len(back_steps))):
+                if k < len(front_steps):
+                    front_steps[k]()
+                if k < len(back_steps):
+                    back_steps[k]()
             if 0 <= s - 2 < NODE_TILES:
                 quantise(s - 2)
-            if 0 <= s - 1 < GATES:
-                regroup_weight(s - 1)
             if 0 <= s - 2 < GATES:
                 quantise_weight(s - 2)
+            if 0 <= s - 1 < GATES:
+                regroup_weight(s - 1)

@@ -39,10 +39,12 @@ def tile_treelstm_pb_v_kernel(
     ) as wraw, tc.tile_pool(name="wgrp", bufs=2 * HALVES) as wgrp, tc.tile_pool(name="work", bufs=2) as work, tc.tile_pool(
         name="grouped", bufs=2 * GATES
     ) as grouped, tc.tile_pool(name="codes", bufs=NODE_TILES) as codes, tc.tile_pool(name="results", bufs=4) as results, tc.psum_pool(
-        name="psum_t", bufs=4
-    ) as psum_t, tc.psum_pool(name="psum_o", bufs=4) as psum_o, tc.manual_schedule():
+        name="psum_t", bufs=GATES
+    ) as psum_t, tc.psum_pool(name="psum_o", bufs=4) as psum_o, tc.psum_pool(name="psum_c", bufs=1) as psum_c, tc.manual_schedule():
         ident = const.tile([P, P], BF16)
         make_identity(nc, ident[:])
+        ident_f32 = const.tile([P, P], F32)
+        make_identity(nc, ident_f32[:])
         w_codes = const.tile([P, GATES, SIZE], U32, align_bytes=64)
         w_scales = const.tile([P, GATES, SIZE], U8, align_bytes=64)
 
@@ -97,7 +99,7 @@ def tile_treelstm_pb_v_kernel(
             gh = g_sb[:, 0:CH]
             u_sq = work.tile([P, CH], F32)
             iu = work.tile([P, CH], F32)
-            cell = work.tile([P, CH], F32)
+            cell = psum_c.tile([P, CH], F32)
             neg_tc = work.tile([P, CH], F32)
             tc_sq = work.tile([P, CH], F32)
             gho = work.tile([P, CH], F32)
@@ -107,16 +109,15 @@ def tile_treelstm_pb_v_kernel(
             kept[n] = (neg_tc, tc_sq, gho, neg_o, neg_i, neg_u)
             nc.scalar.activation(out=u_sq[:], in_=u_sb[:], func=ACT.Square)
 
-            def make_iu():
+            def make_tanh():
                 nc.vector.tensor_tensor(out=iu[:], in0=i_sb[:], in1=u_sb[:], op=ALU.mult)
+                nc.tensor.matmul(out=cell[:], lhsT=ident[:], rhs=fc_sb[:], start=True, stop=False)
+                nc.tensor.matmul(out=cell[:], lhsT=ident_f32[:], rhs=iu[:], start=False, stop=True)
+                nc.scalar.activation(out=neg_tc[:], in_=cell[:], func=ACT.Tanh, scale=-1.0)
+                nc.scalar.activation(out=tc_sq[:], in_=neg_tc[:], func=ACT.Square)
 
             def make_gho():
                 nc.vector.tensor_tensor(out=gho[:], in0=gh, in1=o_sb[:], op=ALU.mult)
-
-            def make_tanh():
-                nc.vector.tensor_tensor(out=cell[:], in0=iu[:], in1=fc_sb[:], op=ALU.add)
-                nc.scalar.activation(out=neg_tc[:], in_=cell[:], func=ACT.Tanh, scale=-1.0)
-                nc.scalar.activation(out=tc_sq[:], in_=neg_tc[:], func=ACT.Square)
 
             def make_neg_o():
                 nc.vector.scalar_tensor_tensor(
@@ -133,7 +134,7 @@ def tile_treelstm_pb_v_kernel(
                     out=neg_u[:], in0=u_sq[:], scalar=1.0, in1=i_sb[:], op0=ALU.subtract, op1=ALU.mult
                 )
 
-            return [make_iu, make_gho, make_tanh, make_neg_o, make_neg_i, make_neg_u]
+            return [make_tanh, make_gho, make_neg_o, make_neg_i, make_neg_u]
 
         def back(n):
             neg_tc, tc_sq, gho, neg_o, neg_i, neg_u = kept[n]

@@ -19,12 +19,14 @@ N_TILE = 512
 NODE_TILES = NODES // P
 HALVES = SIZE // N_TILE
 GATES = 3
-GATE_I, GATE_O, GATE_U = 0, 1, 2
+GATE_O, GATE_I, GATE_U = 0, 1, 2
 
 FLOPS = 2 * NODES * SIZE * CH * GATES
 BYTES = NODES * CH * (2 + 3 * 4) + NODES * 2 * CH * 2 + GATES * CH * SIZE * 2 + NODES * SIZE * 4
 
-FIRST_MULTIPLY_STEP = GATES + 2
+GPSIMD_FROM = NODE_TILES
+CHUNKS = GATES * HALVES
+FIRST_MULTIPLY_STEP = 5
 MULTIPLIES_PER_STEP = 2
 
 
@@ -32,15 +34,15 @@ def tile_treelstm_pb_v_kernel(
     tc, z0, h_tilde, fc_sum, W_i, U_i, b_i, W_o, U_o, b_o, W_u, U_u, b_u, i_j, o_j, u_j, grad_out, out
 ):
     nc = tc.nc
-    weights = (W_i, W_o, W_u)
+    weights = (W_o, W_i, W_u)
 
     with tc.tile_pool(name="const", bufs=1) as const, tc.tile_pool(name="inputs", bufs=NODE_TILES) as inputs, tc.tile_pool(
         name="wraw", bufs=GATES
-    ) as wraw, tc.tile_pool(name="wgrp", bufs=2 * HALVES) as wgrp, tc.tile_pool(name="work", bufs=2) as work, tc.tile_pool(
-        name="grouped", bufs=2 * GATES
-    ) as grouped, tc.tile_pool(name="codes", bufs=NODE_TILES) as codes, tc.tile_pool(name="results", bufs=4) as results, tc.psum_pool(
-        name="psum_t", bufs=GATES
-    ) as psum_t, tc.psum_pool(name="psum_o", bufs=4) as psum_o, tc.psum_pool(name="psum_c", bufs=1) as psum_c, tc.manual_schedule():
+    ) as wraw, tc.tile_pool(name="wgrp", bufs=3) as wgrp, tc.tile_pool(name="single", bufs=1) as single, tc.tile_pool(
+        name="work", bufs=2
+    ) as work, tc.tile_pool(name="ahead", bufs=3) as ahead, tc.tile_pool(name="codes", bufs=NODE_TILES) as codes, tc.tile_pool(
+        name="results", bufs=4
+    ) as results, tc.psum_pool(name="psum_t", bufs=1) as psum_t, tc.psum_pool(name="psum_o", bufs=2) as psum_o, tc.manual_schedule():
         ident = const.tile([P, P], BF16)
         make_identity(nc, ident[:])
         ident_f32 = const.tile([P, P], F32)
@@ -51,189 +53,231 @@ def tile_treelstm_pb_v_kernel(
         loaded = {}
         w_raw = {}
         w_grouped = {}
-        kept = {}
+        squares = {}
+        rows = {}
         turned = {}
-        da_grouped = {}
+        cols = {}
         da_packed = {}
 
         def load_nodes(n):
-            rows = slice(n * P, (n + 1) * P)
+            r = slice(n * P, (n + 1) * P)
             i_sb = inputs.tile([P, CH], F32)
             u_sb = inputs.tile([P, CH], F32)
             g_sb = inputs.tile([P, 2 * CH], BF16)
             o_sb = inputs.tile([P, CH], F32)
             fc_sb = inputs.tile([P, CH], BF16)
-            nc.sync.dma_start(out=i_sb[:], in_=i_j[rows, :])
-            nc.sync.dma_start(out=u_sb[:], in_=u_j[rows, :])
-            nc.sync.dma_start(out=g_sb[:], in_=grad_out[rows, :])
-            nc.sync.dma_start(out=o_sb[:], in_=o_j[rows, :])
-            nc.sync.dma_start(out=fc_sb[:], in_=fc_sum[rows, :])
+            nc.sync.dma_start(out=i_sb[:], in_=i_j[r, :])
+            nc.sync.dma_start(out=u_sb[:], in_=u_j[r, :])
+            nc.sync.dma_start(out=g_sb[:], in_=grad_out[r, :])
+            nc.sync.dma_start(out=o_sb[:], in_=o_j[r, :])
+            nc.sync.dma_start(out=fc_sb[:], in_=fc_sum[r, :])
             loaded[n] = (i_sb, o_sb, u_sb, fc_sb, g_sb)
+            rows[n] = {}
+            turned[n] = {}
+            cols[n] = {}
 
         def load_weight(g):
             raw = wraw.tile([P, PACK, SIZE], BF16)
             nc.sync.dma_start(out=raw[:], in_=weights[g].rearrange("(t p) n -> p t n", p=P))
             w_raw[g] = raw
 
-        def regroup_weight(g):
-            for h in range(HALVES):
-                cols = slice(h * N_TILE, (h + 1) * N_TILE)
-                w_grp = wgrp.tile([P, N_TILE, PACK], BF16, align_bytes=64)
-                nc.scalar.copy(
-                    out=w_grp[:].rearrange("p (c i) t -> p c t i", i=4),
-                    in_=w_raw[g][:, :, cols].rearrange("p t (c i) -> p c t i", i=4),
-                )
-                w_grouped[(g, h)] = w_grp
+        def regroup_chunk(c):
+            g, h = divmod(c, HALVES)
+            w_grp = wgrp.tile([P, N_TILE, PACK], BF16, align_bytes=64)
+            nc.scalar.copy(
+                out=w_grp[:].rearrange("p (c i) t -> p c t i", i=4),
+                in_=w_raw[g][:, :, h * N_TILE : (h + 1) * N_TILE].rearrange("p t (c i) -> p c t i", i=4),
+            )
+            w_grouped[c] = w_grp
 
-        def quantise_weight(g):
-            for h in range(HALVES):
-                cols = slice(h * N_TILE, (h + 1) * N_TILE)
-                nc.vector.quantize_mx(
-                    out=w_codes[:, g, cols].bitcast(E4M3_X4),
-                    scales=w_scales[:, g, cols],
-                    in_=w_grouped[(g, h)][:].rearrange("p n t -> p (n t)"),
-                )
+        def quantise_chunk(c):
+            g, h = divmod(c, HALVES)
+            span = slice(h * N_TILE, (h + 1) * N_TILE)
+            nc.vector.quantize_mx(
+                out=w_codes[:, g, span].bitcast(E4M3_X4),
+                scales=w_scales[:, g, span],
+                in_=w_grouped[c][:].rearrange("p n t -> p (n t)"),
+            )
 
-        def front(n):
+        def square_u(n):
+            u_sq = ahead.tile([P, CH], F32)
+            nc.scalar.activation(out=u_sq[:], in_=loaded[n][2][:], func=ACT.Square)
+            squares[n] = u_sq
+
+        def products(n, engine):
             i_sb, o_sb, u_sb, fc_sb, g_sb = loaded[n]
-            gh = g_sb[:, 0:CH]
-            u_sq = work.tile([P, CH], F32)
-            iu = work.tile([P, CH], F32)
-            cell = psum_c.tile([P, CH], F32)
-            neg_tc = work.tile([P, CH], F32)
-            tc_sq = work.tile([P, CH], F32)
+            iu = single.tile([P, CH], F32)
             gho = work.tile([P, CH], F32)
-            neg_o = work.tile([P, CH], F32)
-            neg_i = work.tile([P, CH], F32)
+            engine.tensor_tensor(out=iu[:], in0=i_sb[:], in1=u_sb[:], op=ALU.mult)
+            engine.tensor_tensor(out=gho[:], in0=g_sb[:, 0:CH], in1=o_sb[:], op=ALU.mult)
+            rows[n]["iu"] = iu
+            rows[n]["gho"] = gho
+
+        def factors(n):
+            i_sb = loaded[n][0]
             neg_u = work.tile([P, CH], F32)
-            kept[n] = (neg_tc, tc_sq, gho, neg_o, neg_i, neg_u)
-            nc.scalar.activation(out=u_sq[:], in_=u_sb[:], func=ACT.Square)
+            neg_i = work.tile([P, CH], F32)
+            nc.vector.scalar_tensor_tensor(
+                out=neg_u[:], in0=squares[n][:], scalar=1.0, in1=i_sb[:], op0=ALU.subtract, op1=ALU.mult
+            )
+            nc.vector.scalar_tensor_tensor(
+                out=neg_i[:], in0=i_sb[:], scalar=1.0, in1=rows[n]["iu"][:], op0=ALU.subtract, op1=ALU.mult
+            )
+            rows[n]["neg_u"] = neg_u
+            rows[n]["neg_i"] = neg_i
 
-            def make_tanh():
-                nc.vector.tensor_tensor(out=iu[:], in0=i_sb[:], in1=u_sb[:], op=ALU.mult)
-                nc.tensor.matmul(out=cell[:], lhsT=ident[:], rhs=fc_sb[:], start=True, stop=False)
-                nc.tensor.matmul(out=cell[:], lhsT=ident_f32[:], rhs=iu[:], start=False, stop=True)
-                nc.scalar.activation(out=neg_tc[:], in_=cell[:], func=ACT.Tanh, scale=-1.0)
-                nc.scalar.activation(out=tc_sq[:], in_=neg_tc[:], func=ACT.Square)
+        def block(t):
+            return slice(t * P, (t + 1) * P)
 
-            def make_gho():
-                nc.vector.tensor_tensor(out=gho[:], in0=gh, in1=o_sb[:], op=ALU.mult)
-
-            def make_neg_o():
-                nc.vector.scalar_tensor_tensor(
-                    out=neg_o[:], in0=o_sb[:], scalar=1.0, in1=gho[:], op0=ALU.subtract, op1=ALU.mult
+        def turn_cell(n):
+            cell_t = psum_t.tile([P, PACK, P], F32)
+            for t in range(PACK):
+                nc.tensor.matmul(out=cell_t[:, t, :], lhsT=loaded[n][3][:, block(t)], rhs=ident[:], start=True, stop=False)
+                nc.tensor.matmul(
+                    out=cell_t[:, t, :], lhsT=rows[n]["iu"][:, block(t)], rhs=ident_f32[:], is_transpose=True, start=False, stop=True
                 )
+            turned[n]["cell"] = cell_t
 
-            def make_neg_i():
-                nc.vector.scalar_tensor_tensor(
-                    out=neg_i[:], in0=i_sb[:], scalar=1.0, in1=iu[:], op0=ALU.subtract, op1=ALU.mult
-                )
+        def tanh(n):
+            neg_tc = work.tile([P, P, PACK], F32)
+            tc_sq = work.tile([P, P, PACK], F32)
+            nc.scalar.activation(out=neg_tc[:], in_=turned[n]["cell"][:].rearrange("p t n -> p n t"), func=ACT.Tanh, scale=-1.0)
+            nc.scalar.activation(out=tc_sq[:], in_=neg_tc[:], func=ACT.Square)
+            cols[n]["neg_tc"] = neg_tc
+            cols[n]["tc_sq"] = tc_sq
 
-            def make_neg_u():
-                nc.vector.scalar_tensor_tensor(
-                    out=neg_u[:], in0=u_sq[:], scalar=1.0, in1=i_sb[:], op0=ALU.subtract, op1=ALU.mult
-                )
+        def turn(n, what, source):
+            turned_tile = psum_t.tile([P, PACK, P], F32, name=what + "_t")
+            for t in range(PACK):
+                nc.tensor.transpose(turned_tile[:, t, :], source[:, block(t)], ident_f32[:])
+            turned[n][what] = turned_tile
 
-            return [make_tanh, make_gho, make_neg_o, make_neg_i, make_neg_u]
+        def turn_gc(n):
+            gc_t = psum_t.tile([P, PACK, P], BF16)
+            for t in range(PACK):
+                nc.tensor.transpose(gc_t[:, t, :], loaded[n][4][:, CH + t * P : CH + (t + 1) * P], ident[:])
+            turned[n]["gc"] = gc_t
 
-        def back(n):
-            neg_tc, tc_sq, gho, neg_o, neg_i, neg_u = kept[n]
-            gc = loaded[n][4][:, CH : 2 * CH]
-            da = work.tile([P, GATES, CH], BF16)
-            neg_dc = work.tile([P, CH], F32)
+        def by_node(n, what):
+            return turned[n][what][:].rearrange("p t n -> p n t")
 
-            def transpose(g):
-                da_t = psum_t.tile([P, PACK, P], BF16)
-                for t in range(PACK):
-                    nc.tensor.transpose(da_t[:, t, :], da[:, g, t * P : (t + 1) * P], ident[:])
-                turned[(n, g)] = da_t
+        def make_masked(n):
+            masked = work.tile([P, P, PACK], F32)
+            nc.vector.scalar_tensor_tensor(
+                out=masked[:], in0=cols[n]["tc_sq"][:], scalar=1.0, in1=by_node(n, "gho"), op0=ALU.subtract, op1=ALU.mult
+            )
+            cols[n]["masked"] = masked
+            cols[n]["da"] = work.tile([P, GATES, P, PACK], BF16, align_bytes=64, name="da")
 
-            def make_da_o():
-                nc.vector.tensor_tensor(out=da[:, GATE_O, :], in0=neg_o[:], in1=neg_tc[:], op=ALU.mult)
-                transpose(GATE_O)
+        def make_x(n):
+            x = work.tile([P, P, PACK], F32)
+            nc.vector.scalar_tensor_tensor(
+                out=x[:], in0=by_node(n, "o"), scalar=1.0, in1=cols[n]["neg_tc"][:], op0=ALU.subtract, op1=ALU.mult
+            )
+            cols[n]["x"] = x
 
-            def make_masked():
-                nc.vector.scalar_tensor_tensor(
-                    out=neg_dc[:], in0=tc_sq[:], scalar=1.0, in1=gho[:], op0=ALU.subtract, op1=ALU.mult
-                )
+        def make_neg_dc(n):
+            neg_dc = work.tile([P, P, PACK], F32)
+            nc.vector.tensor_tensor(out=neg_dc[:], in0=cols[n]["masked"][:], in1=by_node(n, "gc"), op=ALU.subtract)
+            cols[n]["neg_dc"] = neg_dc
 
-            def make_neg_dc():
-                nc.vector.tensor_tensor(out=neg_dc[:], in0=neg_dc[:], in1=gc, op=ALU.subtract)
-
-            def make_da_i():
-                nc.vector.tensor_tensor(out=da[:, GATE_I, :], in0=neg_dc[:], in1=neg_i[:], op=ALU.mult)
-                transpose(GATE_I)
-
-            def make_da_u():
-                nc.vector.tensor_tensor(out=da[:, GATE_U, :], in0=neg_dc[:], in1=neg_u[:], op=ALU.mult)
-                transpose(GATE_U)
-
-            return [make_da_o, make_masked, make_neg_dc, make_da_i, make_da_u]
-
-        def regroup(n):
-            for g in (GATE_O, GATE_I, GATE_U):
-                da_grp = grouped.tile([P, P, PACK], BF16, align_bytes=64)
-                nc.scalar.copy(out=da_grp[:], in_=turned[(n, g)][:].rearrange("p t n -> p n t"))
-                da_grouped[(n, g)] = da_grp
+        def make_da(n, g, left, right):
+            nc.vector.tensor_tensor(out=cols[n]["da"][:, g], in0=cols[n][left][:], in1=by_node(n, right), op=ALU.mult)
 
         def quantise(n):
+            da = cols[n]["da"]
             da_codes = codes.tile([P, GATES, P], U32, align_bytes=64)
             da_scales = codes.tile([P, GATES, P], U8, align_bytes=64)
-            for g in (GATE_O, GATE_I, GATE_U):
-                nc.vector.quantize_mx(
-                    out=da_codes[:, g, :].bitcast(E5M2_X4),
-                    scales=da_scales[:, g, :],
-                    in_=da_grouped[(n, g)][:].rearrange("p n t -> p (n t)"),
-                )
+            nc.vector.quantize_mx(
+                out=da_codes[:, GATE_O, :].bitcast(E5M2_X4),
+                scales=da_scales[:, GATE_O, :],
+                in_=da[:, GATE_O].rearrange("p n t -> p (n t)"),
+            )
+            nc.vector.quantize_mx(
+                out=da_codes[:, GATE_I:GATES, :].rearrange("p g n -> p (g n)").bitcast(E5M2_X4),
+                scales=da_scales[:, GATE_I:GATES, :].rearrange("p g n -> p (g n)"),
+                in_=da[:, GATE_I:GATES].rearrange("p g n t -> p (g n t)"),
+            )
             da_packed[n] = (da_codes, da_scales)
 
         def multiply(n):
             da_codes, da_scales = da_packed[n]
-            acc = [psum_o.tile([P, N_TILE], F32, name="acc") for h in range(HALVES)]
-            for g in range(GATES):
-                for h in range(HALVES):
-                    cols = slice(h * N_TILE, (h + 1) * N_TILE)
+            for h in range(HALVES):
+                span = slice(h * N_TILE, (h + 1) * N_TILE)
+                acc = psum_o.tile([P, N_TILE], F32)
+                for g in range(GATES):
                     nc.tensor.matmul_mx(
-                        out=acc[h][:],
+                        out=acc[:],
                         lhsT=da_codes[:, g, :].bitcast(E5M2_X4),
                         lhsT_scale=da_scales[:, g, :],
-                        rhs=w_codes[:, g, cols].bitcast(E4M3_X4),
-                        rhs_scale=w_scales[:, g, cols],
+                        rhs=w_codes[:, g, span].bitcast(E4M3_X4),
+                        rhs_scale=w_scales[:, g, span],
                         start=(g == 0),
                         stop=(g == GATES - 1),
                     )
-            for h in range(HALVES):
                 result = results.tile([P, N_TILE], F32)
-                nc.scalar.copy(out=result[:], in_=acc[h][:])
-                nc.sync.dma_start(out=out[n * P : (n + 1) * P, h * N_TILE : (h + 1) * N_TILE], in_=result[:])
+                nc.scalar.copy(out=result[:], in_=acc[:])
+                nc.sync.dma_start(out=out[n * P : (n + 1) * P, span], in_=result[:])
 
-        load_nodes(0)
-        load_nodes(1)
+        def is_tile(n):
+            return 0 <= n < NODE_TILES
+
+        for n in range(3):
+            load_nodes(n)
         for g in range(GATES):
             load_weight(g)
-            load_nodes(2 + g)
-        for n in range(2 + GATES, NODE_TILES):
+            load_nodes(3 + g)
+        for n in range(3 + GATES, NODE_TILES):
             load_nodes(n)
 
+        square_u(0)
+        square_u(1)
         multiplied = 0
-        for s in range(NODE_TILES + 3):
-            front_steps = front(s) if s < NODE_TILES else []
-            back_steps = back(s - 1) if 0 <= s - 1 < NODE_TILES else []
-            if 0 <= s - 2 < NODE_TILES:
-                regroup(s - 2)
+        for s in range(-2, NODE_TILES + 2):
+            nxt = s + 1
+            far = s + 2
+            if is_tile(nxt):
+                turn_cell(nxt)
+                tanh(nxt)
             if s >= FIRST_MULTIPLY_STEP:
-                upto = min(s - 2, multiplied + MULTIPLIES_PER_STEP)
+                upto = min(s, NODE_TILES, multiplied + MULTIPLIES_PER_STEP)
                 for n in range(multiplied, upto):
                     multiply(n)
                 multiplied = upto
-            for k in range(max(len(front_steps), len(back_steps))):
-                if k < len(front_steps):
-                    front_steps[k]()
-                if k < len(back_steps):
-                    back_steps[k]()
-            if 0 <= s - 2 < NODE_TILES:
-                quantise(s - 2)
-            if 0 <= s - 2 < GATES:
-                quantise_weight(s - 2)
-            if 0 <= s - 1 < GATES:
-                regroup_weight(s - 1)
+            if is_tile(far + 1):
+                square_u(far + 1)
+            if is_tile(far) and far >= GPSIMD_FROM:
+                products(far, nc.gpsimd)
+            if is_tile(s):
+                make_masked(s)
+                make_x(s)
+            if is_tile(nxt):
+                turn(nxt, "o", loaded[nxt][1])
+            if is_tile(s):
+                make_neg_dc(s)
+            if is_tile(nxt):
+                turn_gc(nxt)
+            if is_tile(s):
+                make_da(s, GATE_O, "x", "gho")
+            if is_tile(nxt):
+                turn(nxt, "gho", rows[nxt]["gho"])
+            if is_tile(s):
+                make_da(s, GATE_I, "neg_dc", "neg_i")
+            if is_tile(nxt):
+                turn(nxt, "neg_i", rows[nxt]["neg_i"])
+            if is_tile(s):
+                make_da(s, GATE_U, "neg_dc", "neg_u")
+            if is_tile(nxt):
+                turn(nxt, "neg_u", rows[nxt]["neg_u"])
+            if is_tile(s):
+                quantise(s)
+            for c in range(CHUNKS):
+                if (2 * c + 1) // 3 + 1 == s:
+                    quantise_chunk(c)
+            if is_tile(far):
+                if far < GPSIMD_FROM:
+                    products(far, nc.vector)
+                factors(far)
+            for c in range(CHUNKS):
+                if (2 * c + 1) // 3 == s:
+                    regroup_chunk(c)

@@ -24,7 +24,7 @@ GATE_O, GATE_I, GATE_U = 0, 1, 2
 FLOPS = 2 * NODES * SIZE * CH * GATES
 BYTES = NODES * CH * (2 + 3 * 4) + NODES * 2 * CH * 2 + GATES * CH * SIZE * 2 + NODES * SIZE * 4
 
-GPSIMD_FROM = NODE_TILES
+GPSIMD_FROM = 2
 CHUNKS = GATES * HALVES
 FIRST_MULTIPLY_STEP = 5
 MULTIPLIES_PER_STEP = 2

@@ -47,6 +47,8 @@ def tile_treelstm_pb_v_kernel(
         make_identity(nc, ident[:])
         ident_f32 = const.tile([P, P], F32)
         make_identity(nc, ident_f32[:])
+        neg_ones = const.tile([P, P], BF16)
+        nc.vector.memset(neg_ones[:], -1.0)
         w_codes = const.tile([P, GATES, SIZE], U32, align_bytes=64)
         w_scales = const.tile([P, GATES, SIZE], U8, align_bytes=64)
 
@@ -152,6 +154,15 @@ def tile_treelstm_pb_v_kernel(
                 nc.tensor.transpose(turned_tile[:, t, :], source[:, block(t)], ident_f32[:])
             turned[n][what] = turned_tile
 
+        def turn_o(n):
+            o_t = psum_t.tile([P, PACK, P], F32)
+            for t in range(PACK):
+                nc.tensor.matmul(out=o_t[:, t, :], lhsT=ident[:], rhs=neg_ones[:], start=True, stop=False)
+                nc.tensor.matmul(
+                    out=o_t[:, t, :], lhsT=loaded[n][1][:, block(t)], rhs=ident_f32[:], is_transpose=True, start=False, stop=True
+                )
+            turned[n]["o"] = o_t
+
         def turn_gc(n):
             gc_t = psum_t.tile([P, PACK, P], BF16)
             for t in range(PACK):
@@ -171,9 +182,7 @@ def tile_treelstm_pb_v_kernel(
 
         def make_x(n):
             x = work.tile([P, P, PACK], F32)
-            nc.vector.scalar_tensor_tensor(
-                out=x[:], in0=by_node(n, "o"), scalar=1.0, in1=cols[n]["neg_tc"][:], op0=ALU.subtract, op1=ALU.mult
-            )
+            nc.vector.tensor_tensor(out=x[:], in0=cols[n]["neg_tc"][:], in1=by_node(n, "o"), op=ALU.mult)
             cols[n]["x"] = x
 
         def make_neg_dc(n):
@@ -252,7 +261,7 @@ def tile_treelstm_pb_v_kernel(
                 make_masked(s)
                 make_x(s)
             if is_tile(nxt):
-                turn(nxt, "o", loaded[nxt][1])
+                turn_o(nxt)
             if is_tile(s):
                 make_neg_dc(s)
             if is_tile(nxt):

@@ -24,10 +24,15 @@ GATE_O, GATE_I, GATE_U = 0, 1, 2
 FLOPS = 2 * NODES * SIZE * CH * GATES
 BYTES = NODES * CH * (2 + 3 * 4) + NODES * 2 * CH * 2 + GATES * CH * SIZE * 2 + NODES * SIZE * 4
 
+FIRST_STEP = -2
 GPSIMD_FROM = 2
 CHUNKS = GATES * HALVES
-FIRST_MULTIPLY_STEP = 5
-MULTIPLIES_PER_STEP = 2
+CHUNK_SHIFT = -1
+MULTIPLIES_PER_STEP = 4
+
+
+def regroup_step(c):
+    return (2 * c + 1) // 3 + CHUNK_SHIFT
 
 
 def tile_treelstm_pb_v_kernel(
@@ -37,7 +42,7 @@ def tile_treelstm_pb_v_kernel(
     weights = (W_o, W_i, W_u)
 
     with tc.tile_pool(name="const", bufs=1) as const, tc.tile_pool(name="inputs", bufs=NODE_TILES) as inputs, tc.tile_pool(
-        name="wraw", bufs=GATES
+        name="wraw", bufs=CHUNKS
     ) as wraw, tc.tile_pool(name="wgrp", bufs=3) as wgrp, tc.tile_pool(name="single", bufs=1) as single, tc.tile_pool(
         name="work", bufs=2
     ) as work, tc.tile_pool(name="ahead", bufs=3) as ahead, tc.tile_pool(name="codes", bufs=NODE_TILES) as codes, tc.tile_pool(
@@ -49,13 +54,12 @@ def tile_treelstm_pb_v_kernel(
         make_identity(nc, ident_f32[:])
         neg_ones = const.tile([P, P], BF16)
         nc.vector.memset(neg_ones[:], -1.0)
-        w_codes = const.tile([P, GATES, SIZE], U32, align_bytes=64)
-        w_scales = const.tile([P, GATES, SIZE], U8, align_bytes=64)
+        w_codes = const.tile([P, CHUNKS, N_TILE], U32, align_bytes=64)
+        w_scales = const.tile([P, CHUNKS, N_TILE], U8, align_bytes=64)
 
         loaded = {}
         w_raw = {}
         w_grouped = {}
-        squares = {}
         rows = {}
         turned = {}
         cols = {}
@@ -70,98 +74,95 @@ def tile_treelstm_pb_v_kernel(
             fc_sb = inputs.tile([P, CH], BF16)
             nc.sync.dma_start(out=i_sb[:], in_=i_j[r, :])
             nc.sync.dma_start(out=u_sb[:], in_=u_j[r, :])
+            nc.sync.dma_start(out=fc_sb[:], in_=fc_sum[r, :])
             nc.sync.dma_start(out=g_sb[:], in_=grad_out[r, :])
             nc.sync.dma_start(out=o_sb[:], in_=o_j[r, :])
-            nc.sync.dma_start(out=fc_sb[:], in_=fc_sum[r, :])
             loaded[n] = (i_sb, o_sb, u_sb, fc_sb, g_sb)
             rows[n] = {}
             turned[n] = {}
             cols[n] = {}
 
-        def load_weight(g):
-            raw = wraw.tile([P, PACK, SIZE], BF16)
-            nc.sync.dma_start(out=raw[:], in_=weights[g].rearrange("(t p) n -> p t n", p=P))
-            w_raw[g] = raw
+        def load_chunk(c):
+            h, g = divmod(c, GATES)
+            raw = wraw.tile([P, PACK, N_TILE], BF16)
+            nc.sync.dma_start(out=raw[:], in_=weights[g][:, h * N_TILE : (h + 1) * N_TILE].rearrange("(t p) n -> p t n", p=P))
+            w_raw[c] = raw
 
         def regroup_chunk(c):
-            g, h = divmod(c, HALVES)
             w_grp = wgrp.tile([P, N_TILE, PACK], BF16, align_bytes=64)
             nc.scalar.copy(
                 out=w_grp[:].rearrange("p (c i) t -> p c t i", i=4),
-                in_=w_raw[g][:, :, h * N_TILE : (h + 1) * N_TILE].rearrange("p t (c i) -> p c t i", i=4),
+                in_=w_raw[c][:].rearrange("p t (c i) -> p c t i", i=4),
             )
             w_grouped[c] = w_grp
 
         def quantise_chunk(c):
-            g, h = divmod(c, HALVES)
-            span = slice(h * N_TILE, (h + 1) * N_TILE)
             nc.vector.quantize_mx(
-                out=w_codes[:, g, span].bitcast(E4M3_X4),
-                scales=w_scales[:, g, span],
+                out=w_codes[:, c, :].bitcast(E4M3_X4),
+                scales=w_scales[:, c, :],
                 in_=w_grouped[c][:].rearrange("p n t -> p (n t)"),
             )
 
         def square_u(n):
             u_sq = ahead.tile([P, CH], F32)
             nc.scalar.activation(out=u_sq[:], in_=loaded[n][2][:], func=ACT.Square)
-            squares[n] = u_sq
+            rows[n]["u_sq"] = u_sq
 
-        def products(n, engine):
-            i_sb, o_sb, u_sb, fc_sb, g_sb = loaded[n]
+        def product_iu(n, engine):
             iu = single.tile([P, CH], F32)
-            gho = work.tile([P, CH], F32)
-            engine.tensor_tensor(out=iu[:], in0=i_sb[:], in1=u_sb[:], op=ALU.mult)
-            engine.tensor_tensor(out=gho[:], in0=g_sb[:, 0:CH], in1=o_sb[:], op=ALU.mult)
+            engine.tensor_tensor(out=iu[:], in0=loaded[n][0][:], in1=loaded[n][2][:], op=ALU.mult)
             rows[n]["iu"] = iu
+
+        def product_gho(n, engine):
+            gho = work.tile([P, CH], F32)
+            engine.tensor_tensor(out=gho[:], in0=loaded[n][4][:, 0:CH], in1=loaded[n][1][:], op=ALU.mult)
             rows[n]["gho"] = gho
 
-        def factors(n):
-            i_sb = loaded[n][0]
+        def factor_u(n):
             neg_u = work.tile([P, CH], F32)
-            neg_i = work.tile([P, CH], F32)
             nc.vector.scalar_tensor_tensor(
-                out=neg_u[:], in0=squares[n][:], scalar=1.0, in1=i_sb[:], op0=ALU.subtract, op1=ALU.mult
-            )
-            nc.vector.scalar_tensor_tensor(
-                out=neg_i[:], in0=i_sb[:], scalar=1.0, in1=rows[n]["iu"][:], op0=ALU.subtract, op1=ALU.mult
+                out=neg_u[:], in0=rows[n]["u_sq"][:], scalar=1.0, in1=loaded[n][0][:], op0=ALU.subtract, op1=ALU.mult
             )
             rows[n]["neg_u"] = neg_u
+
+        def factor_i(n):
+            neg_i = work.tile([P, CH], F32)
+            nc.vector.scalar_tensor_tensor(
+                out=neg_i[:], in0=loaded[n][0][:], scalar=1.0, in1=rows[n]["iu"][:], op0=ALU.subtract, op1=ALU.mult
+            )
             rows[n]["neg_i"] = neg_i
 
         def block(t):
             return slice(t * P, (t + 1) * P)
 
-        def turn_cell(n):
-            cell_t = psum_t.tile([P, PACK, P], F32)
+        def turn_onto(n, what, first_lhsT, first_rhs, source):
+            turned_tile = psum_t.tile([P, PACK, P], F32, name=what + "_t")
             for t in range(PACK):
-                nc.tensor.matmul(out=cell_t[:, t, :], lhsT=loaded[n][3][:, block(t)], rhs=ident[:], start=True, stop=False)
+                nc.tensor.matmul(out=turned_tile[:, t, :], lhsT=first_lhsT(t), rhs=first_rhs, start=True, stop=False)
                 nc.tensor.matmul(
-                    out=cell_t[:, t, :], lhsT=rows[n]["iu"][:, block(t)], rhs=ident_f32[:], is_transpose=True, start=False, stop=True
+                    out=turned_tile[:, t, :], lhsT=source[:, block(t)], rhs=ident_f32[:], is_transpose=True, start=False, stop=True
                 )
-            turned[n]["cell"] = cell_t
+            turned[n][what] = turned_tile
+
+        def turn_cell(n):
+            turn_onto(n, "cell", lambda t: loaded[n][3][:, block(t)], ident[:], rows[n]["iu"])
+
+        def turn_o(n):
+            turn_onto(n, "o", lambda t: ident[:], neg_ones[:], loaded[n][1])
 
         def tanh(n):
-            neg_tc = work.tile([P, P, PACK], F32)
-            tc_sq = work.tile([P, P, PACK], F32)
+            neg_tc = ahead.tile([P, P, PACK], F32)
+            tc_sq = ahead.tile([P, P, PACK], F32)
             nc.scalar.activation(out=neg_tc[:], in_=turned[n]["cell"][:].rearrange("p t n -> p n t"), func=ACT.Tanh, scale=-1.0)
             nc.scalar.activation(out=tc_sq[:], in_=neg_tc[:], func=ACT.Square)
             cols[n]["neg_tc"] = neg_tc
             cols[n]["tc_sq"] = tc_sq
 
-        def turn(n, what, source):
+        def turn(n, what):
             turned_tile = psum_t.tile([P, PACK, P], F32, name=what + "_t")
             for t in range(PACK):
-                nc.tensor.transpose(turned_tile[:, t, :], source[:, block(t)], ident_f32[:])
+                nc.tensor.transpose(turned_tile[:, t, :], rows[n][what][:, block(t)], ident_f32[:])
             turned[n][what] = turned_tile
-
-        def turn_o(n):
-            o_t = psum_t.tile([P, PACK, P], F32)
-            for t in range(PACK):
-                nc.tensor.matmul(out=o_t[:, t, :], lhsT=ident[:], rhs=neg_ones[:], start=True, stop=False)
-                nc.tensor.matmul(
-                    out=o_t[:, t, :], lhsT=loaded[n][1][:, block(t)], rhs=ident_f32[:], is_transpose=True, start=False, stop=True
-                )
-            turned[n]["o"] = o_t
 
         def turn_gc(n):
             gc_t = psum_t.tile([P, PACK, P], BF16)
@@ -209,54 +210,59 @@ def tile_treelstm_pb_v_kernel(
             )
             da_packed[n] = (da_codes, da_scales)
 
-        def multiply(n):
+        def multiply(n, h, on_vector):
             da_codes, da_scales = da_packed[n]
-            for h in range(HALVES):
-                span = slice(h * N_TILE, (h + 1) * N_TILE)
-                acc = psum_o.tile([P, N_TILE], F32)
-                for g in range(GATES):
-                    nc.tensor.matmul_mx(
-                        out=acc[:],
-                        lhsT=da_codes[:, g, :].bitcast(E5M2_X4),
-                        lhsT_scale=da_scales[:, g, :],
-                        rhs=w_codes[:, g, span].bitcast(E4M3_X4),
-                        rhs_scale=w_scales[:, g, span],
-                        start=(g == 0),
-                        stop=(g == GATES - 1),
-                    )
-                result = results.tile([P, N_TILE], F32)
+            acc = psum_o.tile([P, N_TILE], F32)
+            for g in range(GATES):
+                nc.tensor.matmul_mx(
+                    out=acc[:],
+                    lhsT=da_codes[:, g, :].bitcast(E5M2_X4),
+                    lhsT_scale=da_scales[:, g, :],
+                    rhs=w_codes[:, h * GATES + g, :].bitcast(E4M3_X4),
+                    rhs_scale=w_scales[:, h * GATES + g, :],
+                    start=(g == 0),
+                    stop=(g == GATES - 1),
+                )
+            result = results.tile([P, N_TILE], F32)
+            if on_vector:
+                nc.vector.tensor_copy(out=result[:], in_=acc[:])
+            else:
                 nc.scalar.copy(out=result[:], in_=acc[:])
-                nc.sync.dma_start(out=out[n * P : (n + 1) * P, span], in_=result[:])
+            nc.sync.dma_start(out=out[n * P : (n + 1) * P, h * N_TILE : (h + 1) * N_TILE], in_=result[:])
 
         def is_tile(n):
             return 0 <= n < NODE_TILES
 
-        for n in range(3):
-            load_nodes(n)
-        for g in range(GATES):
-            load_weight(g)
-            load_nodes(3 + g)
-        for n in range(3 + GATES, NODE_TILES):
-            load_nodes(n)
+        last_step = NODE_TILES
+        steps = range(FIRST_STEP, last_step + 1)
+
+        for s in steps:
+            if is_tile(s - FIRST_STEP):
+                load_nodes(s - FIRST_STEP)
+            for c in range(CHUNKS):
+                if regroup_step(c) == s:
+                    load_chunk(c)
 
         square_u(0)
-        square_u(1)
-        multiplied = 0
-        for s in range(-2, NODE_TILES + 2):
+        multiplied = [0] * HALVES
+        for s in steps:
             nxt = s + 1
             far = s + 2
-            if is_tile(nxt):
-                turn_cell(nxt)
-                tanh(nxt)
-            if s >= FIRST_MULTIPLY_STEP:
-                upto = min(s, NODE_TILES, multiplied + MULTIPLIES_PER_STEP)
-                for n in range(multiplied, upto):
-                    multiply(n)
-                multiplied = upto
-            if is_tile(far + 1):
-                square_u(far + 1)
-            if is_tile(far) and far >= GPSIMD_FROM:
-                products(far, nc.gpsimd)
+            room = MULTIPLIES_PER_STEP
+            for h in range(HALVES):
+                if s >= regroup_step((h + 1) * GATES - 1) + 2:
+                    upto = min(s, NODE_TILES, multiplied[h] + room)
+                    for n in range(multiplied[h], upto):
+                        multiply(n, h, s == last_step and h == HALVES - 1)
+                    room -= upto - multiplied[h]
+                    multiplied[h] = upto
+            for c in range(CHUNKS):
+                if regroup_step(c) == s:
+                    regroup_chunk(c)
+            if is_tile(far):
+                product_iu(far, nc.gpsimd if far >= GPSIMD_FROM else nc.vector)
+                if far >= GPSIMD_FROM:
+                    product_gho(far, nc.gpsimd)
             if is_tile(s):
                 make_masked(s)
                 make_x(s)
@@ -269,24 +275,27 @@ def tile_treelstm_pb_v_kernel(
             if is_tile(s):
                 make_da(s, GATE_O, "x", "gho")
             if is_tile(nxt):
-                turn(nxt, "gho", rows[nxt]["gho"])
+                turn(nxt, "gho")
+            if is_tile(far):
+                turn_cell(far)
+                tanh(far)
+            if is_tile(far + 1):
+                square_u(far + 1)
             if is_tile(s):
                 make_da(s, GATE_I, "neg_dc", "neg_i")
             if is_tile(nxt):
-                turn(nxt, "neg_i", rows[nxt]["neg_i"])
+                turn(nxt, "neg_i")
             if is_tile(s):
                 make_da(s, GATE_U, "neg_dc", "neg_u")
             if is_tile(nxt):
-                turn(nxt, "neg_u", rows[nxt]["neg_u"])
+                turn(nxt, "neg_u")
             if is_tile(s):
                 quantise(s)
             for c in range(CHUNKS):
-                if (2 * c + 1) // 3 + 1 == s:
+                if regroup_step(c) + 1 == s:
                     quantise_chunk(c)
             if is_tile(far):
+                factor_u(far)
                 if far < GPSIMD_FROM:
-                    products(far, nc.vector)
-                factors(far)
-            for c in range(CHUNKS):
-                if (2 * c + 1) // 3 == s:
-                    regroup_chunk(c)
+                    product_gho(far, nc.vector)
+                factor_i(far)

@@ -52,8 +52,6 @@ def tile_treelstm_pb_v_kernel(
         make_identity(nc, ident[:])
         ident_f32 = const.tile([P, P], F32)
         make_identity(nc, ident_f32[:])
-        neg_ones = const.tile([P, P], BF16)
-        nc.vector.memset(neg_ones[:], -1.0)
         w_codes = const.tile([P, CHUNKS, N_TILE], U32, align_bytes=64)
         w_scales = const.tile([P, CHUNKS, N_TILE], U8, align_bytes=64)
 
@@ -148,7 +146,10 @@ def tile_treelstm_pb_v_kernel(
             turn_onto(n, "cell", lambda t: loaded[n][3][:, block(t)], ident[:], rows[n]["iu"])
 
         def turn_o(n):
-            turn_onto(n, "o", lambda t: ident[:], neg_ones[:], loaded[n][1])
+            o_t = psum_t.tile([P, PACK, P], F32)
+            for t in range(PACK):
+                nc.tensor.transpose(o_t[:, t, :], loaded[n][1][:, block(t)], ident_f32[:])
+            turned[n]["o"] = o_t
 
         def tanh(n):
             neg_tc = ahead.tile([P, P, PACK], F32)
@@ -183,7 +184,9 @@ def tile_treelstm_pb_v_kernel(
 
         def make_x(n):
             x = work.tile([P, P, PACK], F32)
-            nc.vector.tensor_tensor(out=x[:], in0=cols[n]["neg_tc"][:], in1=by_node(n, "o"), op=ALU.mult)
+            nc.vector.scalar_tensor_tensor(
+                out=x[:], in0=by_node(n, "o"), scalar=1.0, in1=cols[n]["neg_tc"][:], op0=ALU.subtract, op1=ALU.mult
+            )
             cols[n]["x"] = x
 
         def make_neg_dc(n):
@@ -295,7 +298,10 @@ def tile_treelstm_pb_v_kernel(
                 if regroup_step(c) + 1 == s:
                     quantise_chunk(c)
             if is_tile(far):
-                factor_u(far)
                 if far < GPSIMD_FROM:
+                    factor_u(far)
                     product_gho(far, nc.vector)
-                factor_i(far)
+                    factor_i(far)
+                else:
+                    factor_i(far)
+                    factor_u(far)

@@ -264,8 +264,7 @@ def tile_treelstm_pb_v_kernel(
                     regroup_chunk(c)
             if is_tile(far):
                 product_iu(far, nc.gpsimd if far >= GPSIMD_FROM else nc.vector)
-                if far >= GPSIMD_FROM:
-                    product_gho(far, nc.gpsimd)
+
             if is_tile(s):
                 make_masked(s)
                 make_x(s)
@@ -303,5 +302,6 @@ def tile_treelstm_pb_v_kernel(
                     product_gho(far, nc.vector)
                     factor_i(far)
                 else:
+                    product_gho(far, nc.vector)
                     factor_i(far)
                     factor_u(far)

@@ -197,41 +197,51 @@ def tile_treelstm_pb_v_kernel(
         def make_da(n, g, left, right):
             nc.vector.tensor_tensor(out=cols[n]["da"][:, g], in0=cols[n][left][:], in1=by_node(n, right), op=ALU.mult)
 
-        def quantise(n):
-            da = cols[n]["da"]
-            da_codes = codes.tile([P, GATES, P], U32, align_bytes=64)
-            da_scales = codes.tile([P, GATES, P], U8, align_bytes=64)
-            nc.vector.quantize_mx(
-                out=da_codes[:, GATE_O, :].bitcast(E5M2_X4),
-                scales=da_scales[:, GATE_O, :],
-                in_=da[:, GATE_O].rearrange("p n t -> p (n t)"),
-            )
-            nc.vector.quantize_mx(
-                out=da_codes[:, GATE_I:GATES, :].rearrange("p g n -> p (g n)").bitcast(E5M2_X4),
-                scales=da_scales[:, GATE_I:GATES, :].rearrange("p g n -> p (g n)"),
-                in_=da[:, GATE_I:GATES].rearrange("p g n t -> p (g n t)"),
-            )
-            da_packed[n] = (da_codes, da_scales)
-
-        def multiply(n, h, on_vector):
+        def quantise(n, first, after):
+            if n not in da_packed:
+                da_codes = codes.tile([P, GATES, P], U32, align_bytes=64)
+                da_scales = codes.tile([P, GATES, P], U8, align_bytes=64)
+                da_packed[n] = (da_codes, da_scales)
             da_codes, da_scales = da_packed[n]
-            acc = psum_o.tile([P, N_TILE], F32)
-            for g in range(GATES):
-                nc.tensor.matmul_mx(
-                    out=acc[:],
-                    lhsT=da_codes[:, g, :].bitcast(E5M2_X4),
-                    lhsT_scale=da_scales[:, g, :],
-                    rhs=w_codes[:, h * GATES + g, :].bitcast(E4M3_X4),
-                    rhs_scale=w_scales[:, h * GATES + g, :],
-                    start=(g == 0),
-                    stop=(g == GATES - 1),
-                )
+            nc.vector.quantize_mx(
+                out=da_codes[:, first:after, :].rearrange("p g n -> p (g n)").bitcast(E5M2_X4),
+                scales=da_scales[:, first:after, :].rearrange("p g n -> p (g n)"),
+                in_=cols[n]["da"][:, first:after].rearrange("p g n t -> p (g n t)"),
+            )
+
+        def one_pass(n, h, g, acc):
+            da_codes, da_scales = da_packed[n]
+            nc.tensor.matmul_mx(
+                out=acc[:],
+                lhsT=da_codes[:, g, :].bitcast(E5M2_X4),
+                lhsT_scale=da_scales[:, g, :],
+                rhs=w_codes[:, h * GATES + g, :].bitcast(E4M3_X4),
+                rhs_scale=w_scales[:, h * GATES + g, :],
+                start=(g == 0),
+                stop=(g == GATES - 1),
+            )
+
+        def store(n, h, acc, on_vector):
             result = results.tile([P, N_TILE], F32)
             if on_vector:
                 nc.vector.tensor_copy(out=result[:], in_=acc[:])
             else:
                 nc.scalar.copy(out=result[:], in_=acc[:])
             nc.sync.dma_start(out=out[n * P : (n + 1) * P, h * N_TILE : (h + 1) * N_TILE], in_=result[:])
+
+        def multiply(n, h):
+            acc = psum_o.tile([P, N_TILE], F32)
+            for g in range(GATES):
+                one_pass(n, h, g, acc)
+            store(n, h, acc, False)
+
+        def multiply_last(n):
+            accs = [psum_o.tile([P, N_TILE], F32, name="acc") for h in range(HALVES)]
+            for g in range(GATES):
+                for h in range(HALVES):
+                    one_pass(n, h, g, accs[h])
+            for h in range(HALVES):
+                store(n, h, accs[h], h == HALVES - 1)
 
         def is_tile(n):
             return 0 <= n < NODE_TILES
@@ -254,11 +264,13 @@ def tile_treelstm_pb_v_kernel(
             room = MULTIPLIES_PER_STEP
             for h in range(HALVES):
                 if s >= regroup_step((h + 1) * GATES - 1) + 2:
-                    upto = min(s, NODE_TILES, multiplied[h] + room)
+                    upto = min(s, NODE_TILES - 1, multiplied[h] + room)
                     for n in range(multiplied[h], upto):
-                        multiply(n, h, s == last_step and h == HALVES - 1)
+                        multiply(n, h)
                     room -= upto - multiplied[h]
                     multiplied[h] = upto
+            if s == last_step:
+                multiply_last(NODE_TILES - 1)
             for c in range(CHUNKS):
                 if regroup_step(c) == s:
                     regroup_chunk(c)
@@ -287,12 +299,18 @@ def tile_treelstm_pb_v_kernel(
                 make_da(s, GATE_I, "neg_dc", "neg_i")
             if is_tile(nxt):
                 turn(nxt, "neg_i")
+            if s == NODE_TILES - 1:
+                quantise(s, GATE_O, GATE_I)
+                quantise(s, GATE_I, GATE_U)
             if is_tile(s):
                 make_da(s, GATE_U, "neg_dc", "neg_u")
             if is_tile(nxt):
                 turn(nxt, "neg_u")
-            if is_tile(s):
-                quantise(s)
+            if s == NODE_TILES - 1:
+                quantise(s, GATE_U, GATES)
+            elif is_tile(s):
+                quantise(s, GATE_O, GATE_I)
+                quantise(s, GATE_I, GATES)
             for c in range(CHUNKS):
                 if regroup_step(c) + 1 == s:
                     quantise_chunk(c)

@@ -27,12 +27,11 @@ BYTES = NODES * CH * (2 + 3 * 4) + NODES * 2 * CH * 2 + GATES * CH * SIZE * 2 + 
 FIRST_STEP = -2
 GPSIMD_FROM = 2
 CHUNKS = GATES * HALVES
-CHUNK_SHIFT = -1
 MULTIPLIES_PER_STEP = 4
 
 
 def regroup_step(c):
-    return (2 * c + 1) // 3 + CHUNK_SHIFT
+    return c + FIRST_STEP
 
 
 def tile_treelstm_pb_v_kernel(
@@ -43,10 +42,10 @@ def tile_treelstm_pb_v_kernel(
 
     with tc.tile_pool(name="const", bufs=1) as const, tc.tile_pool(name="inputs", bufs=NODE_TILES) as inputs, tc.tile_pool(
         name="wraw", bufs=CHUNKS
-    ) as wraw, tc.tile_pool(name="wgrp", bufs=3) as wgrp, tc.tile_pool(name="single", bufs=1) as single, tc.tile_pool(
+    ) as wraw, tc.tile_pool(name="wgrp", bufs=3) as wgrp, tc.tile_pool(name="mixed", bufs=3) as mixed, tc.tile_pool(
         name="work", bufs=2
-    ) as work, tc.tile_pool(name="ahead", bufs=3) as ahead, tc.tile_pool(name="codes", bufs=NODE_TILES) as codes, tc.tile_pool(
-        name="results", bufs=4
+    ) as work, tc.tile_pool(name="codes", bufs=NODE_TILES) as codes, tc.tile_pool(
+        name="results", bufs=6
     ) as results, tc.psum_pool(name="psum_t", bufs=1) as psum_t, tc.psum_pool(name="psum_o", bufs=2) as psum_o, tc.manual_schedule():
         ident = const.tile([P, P], BF16)
         make_identity(nc, ident[:])
@@ -75,7 +74,7 @@ def tile_treelstm_pb_v_kernel(
             nc.sync.dma_start(out=fc_sb[:], in_=fc_sum[r, :])
             nc.sync.dma_start(out=g_sb[:], in_=grad_out[r, :])
             nc.sync.dma_start(out=o_sb[:], in_=o_j[r, :])
-            loaded[n] = (i_sb, o_sb, u_sb, fc_sb, g_sb)
+            loaded[n] = {"i": i_sb, "o": o_sb, "u": u_sb, "fc": fc_sb, "g": g_sb}
             rows[n] = {}
             turned[n] = {}
             cols[n] = {}
@@ -94,6 +93,11 @@ def tile_treelstm_pb_v_kernel(
             )
             w_grouped[c] = w_grp
 
+        def regroup_chunks(s):
+            for c in range(CHUNKS):
+                if regroup_step(c) == s:
+                    regroup_chunk(c)
+
         def quantise_chunk(c):
             nc.vector.quantize_mx(
                 out=w_codes[:, c, :].bitcast(E4M3_X4),
@@ -101,101 +105,87 @@ def tile_treelstm_pb_v_kernel(
                 in_=w_grouped[c][:].rearrange("p n t -> p (n t)"),
             )
 
-        def square_u(n):
-            u_sq = ahead.tile([P, CH], F32)
-            nc.scalar.activation(out=u_sq[:], in_=loaded[n][2][:], func=ACT.Square)
-            rows[n]["u_sq"] = u_sq
-
         def product_iu(n, engine):
-            iu = single.tile([P, CH], F32)
-            engine.tensor_tensor(out=iu[:], in0=loaded[n][0][:], in1=loaded[n][2][:], op=ALU.mult)
+            iu = mixed.tile([P, GATES * P * PACK // 2], F32, offset=0, align_bytes=64)
+            engine.tensor_tensor(out=iu[:, 0:CH], in0=loaded[n]["i"][:], in1=loaded[n]["u"][:], op=ALU.mult)
             rows[n]["iu"] = iu
 
         def product_gho(n, engine):
             gho = work.tile([P, CH], F32)
-            engine.tensor_tensor(out=gho[:], in0=loaded[n][4][:, 0:CH], in1=loaded[n][1][:], op=ALU.mult)
+            engine.tensor_tensor(out=gho[:], in0=loaded[n]["g"][:, 0:CH], in1=loaded[n]["o"][:], op=ALU.mult)
             rows[n]["gho"] = gho
-
-        def factor_u(n):
-            neg_u = work.tile([P, CH], F32)
-            nc.vector.scalar_tensor_tensor(
-                out=neg_u[:], in0=rows[n]["u_sq"][:], scalar=1.0, in1=loaded[n][0][:], op0=ALU.subtract, op1=ALU.mult
-            )
-            rows[n]["neg_u"] = neg_u
-
-        def factor_i(n):
-            neg_i = work.tile([P, CH], F32)
-            nc.vector.scalar_tensor_tensor(
-                out=neg_i[:], in0=loaded[n][0][:], scalar=1.0, in1=rows[n]["iu"][:], op0=ALU.subtract, op1=ALU.mult
-            )
-            rows[n]["neg_i"] = neg_i
 
         def block(t):
             return slice(t * P, (t + 1) * P)
 
-        def turn_onto(n, what, first_lhsT, first_rhs, source):
-            turned_tile = psum_t.tile([P, PACK, P], F32, name=what + "_t")
-            for t in range(PACK):
-                nc.tensor.matmul(out=turned_tile[:, t, :], lhsT=first_lhsT(t), rhs=first_rhs, start=True, stop=False)
-                nc.tensor.matmul(
-                    out=turned_tile[:, t, :], lhsT=source[:, block(t)], rhs=ident_f32[:], is_transpose=True, start=False, stop=True
-                )
-            turned[n][what] = turned_tile
-
         def turn_cell(n):
-            turn_onto(n, "cell", lambda t: loaded[n][3][:, block(t)], ident[:], rows[n]["iu"])
-
-        def turn_o(n):
-            o_t = psum_t.tile([P, PACK, P], F32)
+            cell_t = psum_t.tile([P, PACK, P], F32)
             for t in range(PACK):
-                nc.tensor.transpose(o_t[:, t, :], loaded[n][1][:, block(t)], ident_f32[:])
-            turned[n]["o"] = o_t
+                nc.tensor.matmul(out=cell_t[:, t, :], lhsT=loaded[n]["fc"][:, block(t)], rhs=ident[:], start=True, stop=False)
+                nc.tensor.matmul(
+                    out=cell_t[:, t, :], lhsT=rows[n]["iu"][:, block(t)], rhs=ident_f32[:], is_transpose=True, start=False, stop=True
+                )
+            turned[n]["cell"] = cell_t
 
-        def tanh(n):
-            neg_tc = ahead.tile([P, P, PACK], F32)
-            tc_sq = ahead.tile([P, P, PACK], F32)
-            nc.scalar.activation(out=neg_tc[:], in_=turned[n]["cell"][:].rearrange("p t n -> p n t"), func=ACT.Tanh, scale=-1.0)
-            nc.scalar.activation(out=tc_sq[:], in_=neg_tc[:], func=ACT.Square)
-            cols[n]["neg_tc"] = neg_tc
-            cols[n]["tc_sq"] = tc_sq
-
-        def turn(n, what):
+        def turn(n, what, source):
             turned_tile = psum_t.tile([P, PACK, P], F32, name=what + "_t")
             for t in range(PACK):
-                nc.tensor.transpose(turned_tile[:, t, :], rows[n][what][:, block(t)], ident_f32[:])
+                nc.tensor.transpose(turned_tile[:, t, :], source[:, block(t)], ident_f32[:])
             turned[n][what] = turned_tile
 
         def turn_gc(n):
             gc_t = psum_t.tile([P, PACK, P], BF16)
             for t in range(PACK):
-                nc.tensor.transpose(gc_t[:, t, :], loaded[n][4][:, CH + t * P : CH + (t + 1) * P], ident[:])
+                nc.tensor.transpose(gc_t[:, t, :], loaded[n]["g"][:, CH + t * P : CH + (t + 1) * P], ident[:])
             turned[n]["gc"] = gc_t
 
         def by_node(n, what):
             return turned[n][what][:].rearrange("p t n -> p n t")
 
-        def make_masked(n):
-            masked = work.tile([P, P, PACK], F32)
-            nc.vector.scalar_tensor_tensor(
-                out=masked[:], in0=cols[n]["tc_sq"][:], scalar=1.0, in1=by_node(n, "gho"), op0=ALU.subtract, op1=ALU.mult
-            )
-            cols[n]["masked"] = masked
-            cols[n]["da"] = work.tile([P, GATES, P, PACK], BF16, align_bytes=64, name="da")
+        def new_cols(n, what):
+            tile = work.tile([P, P, PACK], F32, name=what)
+            cols[n][what] = tile
+            return tile[:]
+
+        def tanh(n):
+            nc.scalar.activation(out=new_cols(n, "neg_tc"), in_=by_node(n, "cell"), func=ACT.Tanh, scale=-1.0)
+            nc.scalar.activation(out=new_cols(n, "tc_sq"), in_=cols[n]["neg_tc"][:], func=ACT.Square)
+
+        def square_u(n):
+            nc.scalar.activation(out=new_cols(n, "u_sq"), in_=by_node(n, "u"), func=ACT.Square)
 
         def make_x(n):
-            x = work.tile([P, P, PACK], F32)
             nc.vector.scalar_tensor_tensor(
-                out=x[:], in0=by_node(n, "o"), scalar=1.0, in1=cols[n]["neg_tc"][:], op0=ALU.subtract, op1=ALU.mult
+                out=new_cols(n, "x"), in0=by_node(n, "o"), scalar=1.0, in1=cols[n]["neg_tc"][:], op0=ALU.subtract, op1=ALU.mult
             )
-            cols[n]["x"] = x
+
+        def make_masked(n):
+            nc.vector.scalar_tensor_tensor(
+                out=new_cols(n, "masked"), in0=cols[n]["tc_sq"][:], scalar=1.0, in1=by_node(n, "gho"), op0=ALU.subtract, op1=ALU.mult
+            )
+
+        def make_da_o(n):
+            cols[n]["da"] = mixed.tile([P, GATES, P, PACK], BF16, offset=0, align_bytes=64, name="da")
+            nc.vector.tensor_tensor(out=cols[n]["da"][:, GATE_O], in0=cols[n]["x"][:], in1=by_node(n, "gho"), op=ALU.mult)
 
         def make_neg_dc(n):
-            neg_dc = work.tile([P, P, PACK], F32)
-            nc.vector.tensor_tensor(out=neg_dc[:], in0=cols[n]["masked"][:], in1=by_node(n, "gc"), op=ALU.subtract)
-            cols[n]["neg_dc"] = neg_dc
+            nc.vector.tensor_tensor(out=new_cols(n, "neg_dc"), in0=cols[n]["masked"][:], in1=by_node(n, "gc"), op=ALU.subtract)
 
-        def make_da(n, g, left, right):
-            nc.vector.tensor_tensor(out=cols[n]["da"][:, g], in0=cols[n][left][:], in1=by_node(n, right), op=ALU.mult)
+        def make_q(n):
+            nc.vector.tensor_tensor(out=new_cols(n, "q"), in0=cols[n]["neg_dc"][:], in1=by_node(n, "i"), op=ALU.mult)
+
+        def make_w(n):
+            nc.vector.tensor_tensor(out=new_cols(n, "w"), in0=cols[n]["q"][:], in1=by_node(n, "u"), op=ALU.mult)
+
+        def make_da_i(n):
+            nc.vector.scalar_tensor_tensor(
+                out=cols[n]["da"][:, GATE_I], in0=by_node(n, "i"), scalar=1.0, in1=cols[n]["w"][:], op0=ALU.subtract, op1=ALU.mult
+            )
+
+        def make_da_u(n):
+            nc.vector.scalar_tensor_tensor(
+                out=cols[n]["da"][:, GATE_U], in0=cols[n]["u_sq"][:], scalar=1.0, in1=cols[n]["q"][:], op0=ALU.subtract, op1=ALU.mult
+            )
 
         def quantise(n, first, after):
             if n not in da_packed:
@@ -209,7 +199,7 @@ def tile_treelstm_pb_v_kernel(
                 in_=cols[n]["da"][:, first:after].rearrange("p g n t -> p (g n t)"),
             )
 
-        def one_pass(n, h, g, acc):
+        def one_pass(n, h, g, acc, first, last):
             da_codes, da_scales = da_packed[n]
             nc.tensor.matmul_mx(
                 out=acc[:],
@@ -217,8 +207,8 @@ def tile_treelstm_pb_v_kernel(
                 lhsT_scale=da_scales[:, g, :],
                 rhs=w_codes[:, h * GATES + g, :].bitcast(E4M3_X4),
                 rhs_scale=w_scales[:, h * GATES + g, :],
-                start=(g == 0),
-                stop=(g == GATES - 1),
+                start=first,
+                stop=last,
             )
 
         def store(n, h, acc, on_vector):
@@ -232,14 +222,14 @@ def tile_treelstm_pb_v_kernel(
         def multiply(n, h):
             acc = psum_o.tile([P, N_TILE], F32)
             for g in range(GATES):
-                one_pass(n, h, g, acc)
+                one_pass(n, h, g, acc, g == 0, g == GATES - 1)
             store(n, h, acc, False)
 
         def multiply_last(n):
             accs = [psum_o.tile([P, N_TILE], F32, name="acc") for h in range(HALVES)]
-            for g in range(GATES):
+            for g in (GATE_O, GATE_U, GATE_I):
                 for h in range(HALVES):
-                    one_pass(n, h, g, accs[h])
+                    one_pass(n, h, g, accs[h], g == GATE_O, g == GATE_I)
             for h in range(HALVES):
                 store(n, h, accs[h], h == HALVES - 1)
 
@@ -256,70 +246,78 @@ def tile_treelstm_pb_v_kernel(
                 if regroup_step(c) == s:
                     load_chunk(c)
 
-        square_u(0)
         multiplied = [0] * HALVES
         for s in steps:
             nxt = s + 1
             far = s + 2
-            room = MULTIPLIES_PER_STEP
+            todo = []
             for h in range(HALVES):
                 if s >= regroup_step((h + 1) * GATES - 1) + 2:
-                    upto = min(s, NODE_TILES - 1, multiplied[h] + room)
-                    for n in range(multiplied[h], upto):
-                        multiply(n, h)
-                    room -= upto - multiplied[h]
+                    upto = min(s, NODE_TILES - 1, multiplied[h] + MULTIPLIES_PER_STEP - len(todo))
+                    todo += [(n, h) for n in range(multiplied[h], upto)]
                     multiplied[h] = upto
+            early = (len(todo) + 1) // 2
+            engine = nc.gpsimd if far >= GPSIMD_FROM else nc.vector
+
+            for n, h in todo[:early]:
+                multiply(n, h)
             if s == last_step:
                 multiply_last(NODE_TILES - 1)
-            for c in range(CHUNKS):
-                if regroup_step(c) == s:
-                    regroup_chunk(c)
-            if is_tile(far):
-                product_iu(far, nc.gpsimd if far >= GPSIMD_FROM else nc.vector)
-
+            if s >= 0:
+                regroup_chunks(s)
+            if is_tile(far) and far != 1:
+                product_iu(far, engine)
+                if far < GPSIMD_FROM:
+                    turn_cell(far)
+                    tanh(far)
             if is_tile(s):
-                make_masked(s)
-                make_x(s)
+                make_q(s)
             if is_tile(nxt):
-                turn_o(nxt)
+                make_x(nxt)
+            if is_tile(far) and far >= GPSIMD_FROM:
+                turn(far, "o", loaded[far]["o"])
             if is_tile(s):
-                make_neg_dc(s)
+                make_w(s)
             if is_tile(nxt):
-                turn_gc(nxt)
-            if is_tile(s):
-                make_da(s, GATE_O, "x", "gho")
-            if is_tile(nxt):
-                turn(nxt, "gho")
-            if is_tile(far):
+                turn(nxt, "u", loaded[nxt]["u"])
+                make_masked(nxt)
+            if far == 1:
+                product_iu(far, engine)
                 turn_cell(far)
                 tanh(far)
-            if is_tile(far + 1):
-                square_u(far + 1)
-            if is_tile(s):
-                make_da(s, GATE_I, "neg_dc", "neg_i")
             if is_tile(nxt):
-                turn(nxt, "neg_i")
+                square_u(nxt)
+            if is_tile(far) and far >= GPSIMD_FROM:
+                turn_cell(far)
+                tanh(far)
             if s == NODE_TILES - 1:
-                quantise(s, GATE_O, GATE_I)
-                quantise(s, GATE_I, GATE_U)
-            if is_tile(s):
-                make_da(s, GATE_U, "neg_dc", "neg_u")
-            if is_tile(nxt):
-                turn(nxt, "neg_u")
-            if s == NODE_TILES - 1:
+                make_da_u(s)
+                make_da_i(s)
                 quantise(s, GATE_U, GATES)
+                quantise(s, GATE_I, GATE_U)
             elif is_tile(s):
-                quantise(s, GATE_O, GATE_I)
+                make_da_i(s)
+            if is_tile(nxt):
+                turn(nxt, "i", loaded[nxt]["i"])
+                make_da_o(nxt)
+            if is_tile(far) and far < GPSIMD_FROM:
+                turn(far, "o", loaded[far]["o"])
+                regroup_chunks(s)
+            for n, h in todo[early:]:
+                multiply(n, h)
+            if is_tile(far):
+                product_gho(far, engine)
+                turn(far, "gho", rows[far]["gho"])
+            if is_tile(nxt):
+                make_neg_dc(nxt)
+            if is_tile(far):
+                turn_gc(far)
+            if is_tile(s) and s < NODE_TILES - 1:
+                make_da_u(s)
+            if is_tile(nxt):
+                quantise(nxt, GATE_O, GATE_I)
+            if is_tile(s) and s < NODE_TILES - 1:
                 quantise(s, GATE_I, GATES)
             for c in range(CHUNKS):
                 if regroup_step(c) + 1 == s:
                     quantise_chunk(c)
-            if is_tile(far):
-                if far < GPSIMD_FROM:
-                    factor_u(far)
-                    product_gho(far, nc.vector)
-                    factor_i(far)
-                else:
-                    product_gho(far, nc.vector)
-                    factor_i(far)
-                    factor_u(far)

@@ -118,14 +118,22 @@ def tile_treelstm_pb_v_kernel(
         def block(t):
             return slice(t * P, (t + 1) * P)
 
-        def turn_cell(n):
+        def turn_fc(n):
             cell_t = psum_t.tile([P, PACK, P], F32)
             for t in range(PACK):
-                nc.tensor.matmul(out=cell_t[:, t, :], lhsT=loaded[n]["fc"][:, block(t)], rhs=ident[:], start=True, stop=False)
-                nc.tensor.matmul(
-                    out=cell_t[:, t, :], lhsT=rows[n]["iu"][:, block(t)], rhs=ident_f32[:], is_transpose=True, start=False, stop=True
-                )
+                nc.tensor.matmul(out=cell_t[:, t, :], lhsT=loaded[n]["fc"][:, block(t)], rhs=ident[:], start=(t == 0), stop=False)
             turned[n]["cell"] = cell_t
+
+        def turn_cell(n):
+            for t in range(PACK):
+                nc.tensor.matmul(
+                    out=turned[n]["cell"][:, t, :],
+                    lhsT=rows[n]["iu"][:, block(t)],
+                    rhs=ident_f32[:],
+                    is_transpose=True,
+                    start=False,
+                    stop=(t == PACK - 1),
+                )
 
         def turn(n, what, source):
             turned_tile = psum_t.tile([P, PACK, P], F32, name=what + "_t")
@@ -268,8 +276,11 @@ def tile_treelstm_pb_v_kernel(
             if is_tile(far) and far != 1:
                 product_iu(far, engine)
                 if far < GPSIMD_FROM:
+                    turn_fc(far)
                     turn_cell(far)
                     tanh(far)
+                else:
+                    turn_fc(far)
             if is_tile(s):
                 make_q(s)
             if is_tile(nxt):
@@ -283,6 +294,7 @@ def tile_treelstm_pb_v_kernel(
                 make_masked(nxt)
             if far == 1:
                 product_iu(far, engine)
+                turn_fc(far)
                 turn_cell(far)
                 tanh(far)
             if is_tile(nxt):
@@ -314,10 +326,10 @@ def tile_treelstm_pb_v_kernel(
                 turn_gc(far)
             if is_tile(s) and s < NODE_TILES - 1:
                 make_da_u(s)
+            for c in range(CHUNKS):
+                if regroup_step(c) + 1 == s:
+                    quantise_chunk(c)
             if is_tile(nxt):
                 quantise(nxt, GATE_O, GATE_I)
             if is_tile(s) and s < NODE_TILES - 1:
                 quantise(s, GATE_I, GATES)
-            for c in range(CHUNKS):
-                if regroup_step(c) + 1 == s:
-                    quantise_chunk(c)

@@ -25,7 +25,6 @@ FLOPS = 2 * NODES * SIZE * CH * GATES
 BYTES = NODES * CH * (2 + 3 * 4) + NODES * 2 * CH * 2 + GATES * CH * SIZE * 2 + NODES * SIZE * 4
 
 FIRST_STEP = -2
-GPSIMD_FROM = 2
 CHUNKS = GATES * HALVES
 MULTIPLIES_PER_STEP = 4
 
@@ -44,7 +43,7 @@ def tile_treelstm_pb_v_kernel(
         name="wraw", bufs=CHUNKS
     ) as wraw, tc.tile_pool(name="wgrp", bufs=3) as wgrp, tc.tile_pool(name="mixed", bufs=3) as mixed, tc.tile_pool(
         name="work", bufs=2
-    ) as work, tc.tile_pool(name="codes", bufs=NODE_TILES) as codes, tc.tile_pool(
+    ) as work, tc.tile_pool(name="single", bufs=1) as single, tc.tile_pool(name="ahead", bufs=3) as ahead, tc.tile_pool(name="codes", bufs=NODE_TILES) as codes, tc.tile_pool(
         name="results", bufs=6
     ) as results, tc.psum_pool(name="psum_t", bufs=1) as psum_t, tc.psum_pool(name="psum_o", bufs=2) as psum_o, tc.manual_schedule():
         ident = const.tile([P, P], BF16)
@@ -106,13 +105,13 @@ def tile_treelstm_pb_v_kernel(
             )
 
         def product_iu(n, engine):
-            iu = mixed.tile([P, GATES * P * PACK // 2], F32, offset=0, align_bytes=64)
-            engine.tensor_tensor(out=iu[:, 0:CH], in0=loaded[n]["i"][:], in1=loaded[n]["u"][:], op=ALU.mult)
+            iu = single.tile([P, CH], F32)
+            engine.tensor_tensor(out=iu[:], in0=loaded[n]["i"][:], in1=loaded[n]["u"][:], op=ALU.mult)
             rows[n]["iu"] = iu
 
         def product_gho(n, engine):
-            gho = work.tile([P, CH], F32)
-            engine.tensor_tensor(out=gho[:], in0=loaded[n]["g"][:, 0:CH], in1=loaded[n]["o"][:], op=ALU.mult)
+            gho = mixed.tile([P, GATES * P * PACK // 2], F32, offset=0, align_bytes=64)
+            engine.tensor_tensor(out=gho[:, 0:CH], in0=loaded[n]["g"][:, 0:CH], in1=loaded[n]["o"][:], op=ALU.mult)
             rows[n]["gho"] = gho
 
         def block(t):
@@ -142,34 +141,35 @@ def tile_treelstm_pb_v_kernel(
             turned[n][what] = turned_tile
 
         def turn_gc(n):
-            gc_t = psum_t.tile([P, PACK, P], BF16)
+            gc_t = psum_t.tile([P, PACK, P], F32)
             for t in range(PACK):
-                nc.tensor.transpose(gc_t[:, t, :], loaded[n]["g"][:, CH + t * P : CH + (t + 1) * P], ident[:])
+                gc = loaded[n]["g"][:, CH + t * P : CH + (t + 1) * P]
+                nc.tensor.matmul(out=gc_t[:, t, :], lhsT=gc, rhs=ident[:], start=(t == 0), stop=(t == PACK - 1))
             turned[n]["gc"] = gc_t
 
         def by_node(n, what):
             return turned[n][what][:].rearrange("p t n -> p n t")
 
-        def new_cols(n, what):
-            tile = work.tile([P, P, PACK], F32, name=what)
+        def new_cols(n, what, pool):
+            tile = pool.tile([P, P, PACK], F32, name=what)
             cols[n][what] = tile
             return tile[:]
 
         def tanh(n):
-            nc.scalar.activation(out=new_cols(n, "neg_tc"), in_=by_node(n, "cell"), func=ACT.Tanh, scale=-1.0)
-            nc.scalar.activation(out=new_cols(n, "tc_sq"), in_=cols[n]["neg_tc"][:], func=ACT.Square)
+            nc.scalar.activation(out=new_cols(n, "neg_tc", ahead), in_=by_node(n, "cell"), func=ACT.Tanh, scale=-1.0)
+            nc.scalar.activation(out=new_cols(n, "tc_sq", ahead), in_=cols[n]["neg_tc"][:], func=ACT.Square)
 
         def square_u(n):
-            nc.scalar.activation(out=new_cols(n, "u_sq"), in_=by_node(n, "u"), func=ACT.Square)
+            nc.scalar.activation(out=new_cols(n, "u_sq", work), in_=by_node(n, "u"), func=ACT.Square)
 
         def make_x(n):
             nc.vector.scalar_tensor_tensor(
-                out=new_cols(n, "x"), in0=by_node(n, "o"), scalar=1.0, in1=cols[n]["neg_tc"][:], op0=ALU.subtract, op1=ALU.mult
+                out=new_cols(n, "x", work), in0=by_node(n, "o"), scalar=1.0, in1=cols[n]["neg_tc"][:], op0=ALU.subtract, op1=ALU.mult
             )
 
         def make_masked(n):
             nc.vector.scalar_tensor_tensor(
-                out=new_cols(n, "masked"), in0=cols[n]["tc_sq"][:], scalar=1.0, in1=by_node(n, "gho"), op0=ALU.subtract, op1=ALU.mult
+                out=new_cols(n, "masked", work), in0=cols[n]["tc_sq"][:], scalar=1.0, in1=by_node(n, "gho"), op0=ALU.subtract, op1=ALU.mult
             )
 
         def make_da_o(n):
@@ -177,13 +177,13 @@ def tile_treelstm_pb_v_kernel(
             nc.vector.tensor_tensor(out=cols[n]["da"][:, GATE_O], in0=cols[n]["x"][:], in1=by_node(n, "gho"), op=ALU.mult)
 
         def make_neg_dc(n):
-            nc.vector.tensor_tensor(out=new_cols(n, "neg_dc"), in0=cols[n]["masked"][:], in1=by_node(n, "gc"), op=ALU.subtract)
+            nc.vector.tensor_tensor(out=new_cols(n, "neg_dc", work), in0=cols[n]["masked"][:], in1=by_node(n, "gc"), op=ALU.subtract)
 
         def make_q(n):
-            nc.vector.tensor_tensor(out=new_cols(n, "q"), in0=cols[n]["neg_dc"][:], in1=by_node(n, "i"), op=ALU.mult)
+            nc.vector.tensor_tensor(out=new_cols(n, "q", work), in0=cols[n]["neg_dc"][:], in1=by_node(n, "i"), op=ALU.mult)
 
         def make_w(n):
-            nc.vector.tensor_tensor(out=new_cols(n, "w"), in0=cols[n]["q"][:], in1=by_node(n, "u"), op=ALU.mult)
+            nc.vector.tensor_tensor(out=new_cols(n, "w", work), in0=cols[n]["q"][:], in1=by_node(n, "u"), op=ALU.mult)
 
         def make_da_i(n):
             nc.vector.scalar_tensor_tensor(
@@ -233,19 +233,20 @@ def tile_treelstm_pb_v_kernel(
                 one_pass(n, h, g, acc, g == 0, g == GATES - 1)
             store(n, h, acc, False)
 
-        def multiply_last(n):
-            accs = [psum_o.tile([P, N_TILE], F32, name="acc") for h in range(HALVES)]
-            for g in (GATE_O, GATE_U, GATE_I):
-                for h in range(HALVES):
-                    one_pass(n, h, g, accs[h], g == GATE_O, g == GATE_I)
+        def multiply_gate(n, g, accs, first, last):
             for h in range(HALVES):
-                store(n, h, accs[h], h == HALVES - 1)
+                one_pass(n, h, g, accs[h], first, last)
+
+        def start_tile(n):
+            product_iu(n, nc.vector)
+            turn_fc(n)
+            turn_cell(n)
+            tanh(n)
 
         def is_tile(n):
             return 0 <= n < NODE_TILES
 
-        last_step = NODE_TILES
-        steps = range(FIRST_STEP, last_step + 1)
+        steps = range(FIRST_STEP, NODE_TILES)
 
         for s in steps:
             if is_tile(s - FIRST_STEP):
@@ -265,43 +266,43 @@ def tile_treelstm_pb_v_kernel(
                     todo += [(n, h) for n in range(multiplied[h], upto)]
                     multiplied[h] = upto
             early = (len(todo) + 1) // 2
-            engine = nc.gpsimd if far >= GPSIMD_FROM else nc.vector
-
-            for n, h in todo[:early]:
-                multiply(n, h)
-            if s == last_step:
-                multiply_last(NODE_TILES - 1)
             if s >= 0:
                 regroup_chunks(s)
-            if is_tile(far) and far != 1:
-                product_iu(far, engine)
-                if far < GPSIMD_FROM:
-                    turn_fc(far)
-                    turn_cell(far)
-                    tanh(far)
-                else:
-                    turn_fc(far)
+            if s == FIRST_STEP:
+                start_tile(far)
+                turn(far, "o", loaded[far]["o"])
+            if is_tile(nxt):
+                turn_gc(nxt)
+            if is_tile(far) and s >= 0:
+                turn_fc(far)
+            if s == NODE_TILES - 1:
+                last_accs = [psum_t.tile([P, N_TILE], F32, name=what + "_t") for what in ("cell", "o")]
+                multiply_gate(s, GATE_O, last_accs, True, False)
+            for n, h in todo[:early]:
+                multiply(n, h)
+            if is_tile(far) and s >= 0:
+                turn_cell(far)
+                tanh(far)
+                product_gho(far, nc.gpsimd)
             if is_tile(s):
                 make_q(s)
             if is_tile(nxt):
                 make_x(nxt)
-            if is_tile(far) and far >= GPSIMD_FROM:
+            if is_tile(far) and s >= 0:
                 turn(far, "o", loaded[far]["o"])
             if is_tile(s):
                 make_w(s)
             if is_tile(nxt):
                 turn(nxt, "u", loaded[nxt]["u"])
-                make_masked(nxt)
-            if far == 1:
-                product_iu(far, engine)
-                turn_fc(far)
-                turn_cell(far)
-                tanh(far)
-            if is_tile(nxt):
                 square_u(nxt)
-            if is_tile(far) and far >= GPSIMD_FROM:
-                turn_cell(far)
-                tanh(far)
+                make_masked(nxt)
+            if is_tile(far) and FIRST_STEP < s < 0:
+                start_tile(far)
+                turn(far, "o", loaded[far]["o"])
+            if s >= -1 and is_tile(far + 1) and s != 0:
+                product_iu(far + 1, nc.gpsimd)
+            if s < 0:
+                regroup_chunks(s)
             if s == NODE_TILES - 1:
                 make_da_u(s)
                 make_da_i(s)
@@ -312,18 +313,14 @@ def tile_treelstm_pb_v_kernel(
             if is_tile(nxt):
                 turn(nxt, "i", loaded[nxt]["i"])
                 make_da_o(nxt)
-            if is_tile(far) and far < GPSIMD_FROM:
-                turn(far, "o", loaded[far]["o"])
-                regroup_chunks(s)
+            if is_tile(far):
+                if s < 0:
+                    product_gho(far, nc.vector)
+                turn(far, "gho", rows[far]["gho"])
             for n, h in todo[early:]:
                 multiply(n, h)
-            if is_tile(far):
-                product_gho(far, engine)
-                turn(far, "gho", rows[far]["gho"])
             if is_tile(nxt):
                 make_neg_dc(nxt)
-            if is_tile(far):
-                turn_gc(far)
             if is_tile(s) and s < NODE_TILES - 1:
                 make_da_u(s)
             for c in range(CHUNKS):
@@ -333,3 +330,10 @@ def tile_treelstm_pb_v_kernel(
                 quantise(nxt, GATE_O, GATE_I)
             if is_tile(s) and s < NODE_TILES - 1:
                 quantise(s, GATE_I, GATES)
+            if s == 0:
+                product_iu(far + 1, nc.vector)
+
+        multiply_gate(NODE_TILES - 1, GATE_U, last_accs, False, False)
+        multiply_gate(NODE_TILES - 1, GATE_I, last_accs, False, True)
+        for h in range(HALVES):
+            store(NODE_TILES - 1, h, last_accs[h], h == HALVES - 1)

@@ -17,6 +17,7 @@ CH = 512
 SIZE = 1024
 N_TILE = 512
 NODE_TILES = NODES // P
+LAST = NODE_TILES - 1
 HALVES = SIZE // N_TILE
 GATES = 3
 GATE_O, GATE_I, GATE_U = 0, 1, 2
@@ -27,10 +28,12 @@ BYTES = NODES * CH * (2 + 3 * 4) + NODES * 2 * CH * 2 + GATES * CH * SIZE * 2 + 
 FIRST_STEP = -2
 CHUNKS = GATES * HALVES
 MULTIPLIES_PER_STEP = 4
+BY_GATE = (LAST - 1, LAST)
+LAST_PARTS = 2
 
 
 def regroup_step(c):
-    return c + FIRST_STEP
+    return min(c, CHUNKS - 2) + FIRST_STEP
 
 
 def tile_treelstm_pb_v_kernel(
@@ -92,8 +95,8 @@ def tile_treelstm_pb_v_kernel(
             )
             w_grouped[c] = w_grp
 
-        def regroup_chunks(s):
-            for c in range(CHUNKS):
+        def regroup_chunks(s, upto):
+            for c in range(upto):
                 if regroup_step(c) == s:
                     regroup_chunk(c)
 
@@ -110,7 +113,7 @@ def tile_treelstm_pb_v_kernel(
             rows[n]["iu"] = iu
 
         def product_gho(n, engine):
-            gho = mixed.tile([P, GATES * P * PACK // 2], F32, offset=0, align_bytes=64)
+            gho = mixed.tile([P, GATES * P * PACK // 2], F32, offset=0, align_bytes=64, name="gho")
             engine.tensor_tensor(out=gho[:, 0:CH], in0=loaded[n]["g"][:, 0:CH], in1=loaded[n]["o"][:], op=ALU.mult)
             rows[n]["gho"] = gho
 
@@ -134,11 +137,11 @@ def tile_treelstm_pb_v_kernel(
                     stop=(t == PACK - 1),
                 )
 
-        def turn(n, what, source):
-            turned_tile = psum_t.tile([P, PACK, P], F32, name=what + "_t")
+        def turn(n, bank, source, what=None):
+            turned_tile = psum_t.tile([P, PACK, P], F32, name=bank + "_t")
             for t in range(PACK):
                 nc.tensor.transpose(turned_tile[:, t, :], source[:, block(t)], ident_f32[:])
-            turned[n][what] = turned_tile
+            turned[n][what or bank] = turned_tile
 
         def turn_gc(n):
             gc_t = psum_t.tile([P, PACK, P], F32)
@@ -195,6 +198,29 @@ def tile_treelstm_pb_v_kernel(
                 out=cols[n]["da"][:, GATE_U], in0=cols[n]["u_sq"][:], scalar=1.0, in1=cols[n]["q"][:], op0=ALU.subtract, op1=ALU.mult
             )
 
+        def prepare_factors(n):
+            i_1 = single.tile([P, CH], F32)
+            u_sq = single.tile([P, CH], F32, name="u_sq_rows")
+            u_sq_1 = single.tile([P, CH], F32)
+            nc.scalar.activation(out=i_1[:], in_=loaded[n]["i"][:], func=ACT.Identity, bias=-1.0)
+            nc.scalar.activation(out=u_sq[:], in_=loaded[n]["u"][:], func=ACT.Square)
+            nc.scalar.activation(out=u_sq_1[:], in_=u_sq[:], func=ACT.Identity, bias=-1.0)
+            rows[n]["i_1"] = i_1
+            rows[n]["u_sq_1"] = u_sq_1
+
+        def factor_i(n):
+            neg_i = single.tile([P, CH], F32)
+            nc.gpsimd.tensor_tensor(out=neg_i[:], in0=rows[n]["i_1"][:], in1=rows[n]["iu"][:], op=ALU.mult)
+            rows[n]["neg_i"] = neg_i
+
+        def factor_u(n):
+            neg_u = mixed.tile([P, GATES * P * PACK // 2], F32, offset=0, align_bytes=64, name="gho")
+            nc.gpsimd.tensor_tensor(out=neg_u[:, 0:CH], in0=rows[n]["u_sq_1"][:], in1=loaded[n]["i"][:], op=ALU.mult)
+            rows[n]["neg_u"] = neg_u
+
+        def make_last_da(n, gate, factor):
+            nc.vector.tensor_tensor(out=cols[n]["da"][:, gate], in0=cols[n]["neg_dc"][:], in1=by_node(n, factor), op=ALU.mult)
+
         def quantise(n, first, after):
             if n not in da_packed:
                 da_codes = codes.tile([P, GATES, P], U32, align_bytes=64)
@@ -219,19 +245,23 @@ def tile_treelstm_pb_v_kernel(
                 stop=last,
             )
 
-        def store(n, h, acc, on_vector):
+        def store(n, h, acc):
             result = results.tile([P, N_TILE], F32)
-            if on_vector:
-                nc.vector.tensor_copy(out=result[:], in_=acc[:])
-            else:
-                nc.scalar.copy(out=result[:], in_=acc[:])
+            nc.scalar.copy(out=result[:], in_=acc[:])
             nc.sync.dma_start(out=out[n * P : (n + 1) * P, h * N_TILE : (h + 1) * N_TILE], in_=result[:])
+
+        def store_part(n, h, acc, part, copy):
+            width = N_TILE // LAST_PARTS
+            result = single.tile([P, width], F32, name="last_%d_%d" % (h, part))
+            copy(out=result[:], in_=acc[:, part * width : (part + 1) * width])
+            first = h * N_TILE + part * width
+            nc.sync.dma_start(out=out[n * P : (n + 1) * P, first : first + width], in_=result[:])
 
         def multiply(n, h):
             acc = psum_o.tile([P, N_TILE], F32)
             for g in range(GATES):
                 one_pass(n, h, g, acc, g == 0, g == GATES - 1)
-            store(n, h, acc, False)
+            store(n, h, acc)
 
         def multiply_gate(n, g, accs, first, last):
             for h in range(HALVES):
@@ -262,12 +292,13 @@ def tile_treelstm_pb_v_kernel(
             todo = []
             for h in range(HALVES):
                 if s >= regroup_step((h + 1) * GATES - 1) + 2:
-                    upto = min(s, NODE_TILES - 1, multiplied[h] + MULTIPLIES_PER_STEP - len(todo))
+                    upto = min(s, BY_GATE[0], multiplied[h] + MULTIPLIES_PER_STEP - len(todo))
                     todo += [(n, h) for n in range(multiplied[h], upto)]
                     multiplied[h] = upto
             early = (len(todo) + 1) // 2
+            middle = early + (len(todo) - early) // 2
             if s >= 0:
-                regroup_chunks(s)
+                regroup_chunks(s, CHUNKS - 1)
             if s == FIRST_STEP:
                 start_tile(far)
                 turn(far, "o", loaded[far]["o"])
@@ -275,26 +306,37 @@ def tile_treelstm_pb_v_kernel(
                 turn_gc(nxt)
             if is_tile(far) and s >= 0:
                 turn_fc(far)
-            if s == NODE_TILES - 1:
-                last_accs = [psum_t.tile([P, N_TILE], F32, name=what + "_t") for what in ("cell", "o")]
-                multiply_gate(s, GATE_O, last_accs, True, False)
+            if s == LAST:
+                accs[s] = [psum_t.tile([P, N_TILE], F32, name=what + "_t") for what in ("cell", "o")]
+                multiply_gate(s, GATE_O, accs[s], True, False)
+                multiply_gate(s - 1, GATE_I, accs[s - 1], False, False)
+                multiply_gate(s - 1, GATE_U, accs[s - 1], False, True)
+                for h in range(HALVES):
+                    store(s - 1, h, accs[s - 1][h])
             for n, h in todo[:early]:
                 multiply(n, h)
             if is_tile(far) and s >= 0:
                 turn_cell(far)
                 tanh(far)
                 product_gho(far, nc.gpsimd)
-            if is_tile(s):
+            if far == LAST:
+                factor_i(far)
+            if nxt == LAST:
+                factor_u(nxt)
+            if is_tile(s) and s != LAST:
                 make_q(s)
             if is_tile(nxt):
                 make_x(nxt)
             if is_tile(far) and s >= 0:
                 turn(far, "o", loaded[far]["o"])
-            if is_tile(s):
+            if is_tile(s) and s != LAST:
                 make_w(s)
             if is_tile(nxt):
-                turn(nxt, "u", loaded[nxt]["u"])
-                square_u(nxt)
+                if nxt == LAST:
+                    turn(nxt, "u", rows[nxt]["neg_i"], "neg_i")
+                else:
+                    turn(nxt, "u", loaded[nxt]["u"])
+                    square_u(nxt)
                 make_masked(nxt)
             if is_tile(far) and FIRST_STEP < s < 0:
                 start_tile(far)
@@ -302,38 +344,51 @@ def tile_treelstm_pb_v_kernel(
             if s >= -1 and is_tile(far + 1) and s != 0:
                 product_iu(far + 1, nc.gpsimd)
             if s < 0:
-                regroup_chunks(s)
-            if s == NODE_TILES - 1:
-                make_da_u(s)
+                regroup_chunks(s, CHUNKS - 1)
+            if s == regroup_step(CHUNKS - 1):
+                regroup_chunk(CHUNKS - 1)
+            if is_tile(s) and s != LAST:
                 make_da_i(s)
-                quantise(s, GATE_U, GATES)
+            if s == LAST:
+                make_last_da(s, GATE_I, "neg_i")
+                make_last_da(s, GATE_U, "neg_u")
                 quantise(s, GATE_I, GATE_U)
-            elif is_tile(s):
-                make_da_i(s)
+                quantise(s, GATE_U, GATES)
+            for n, h in todo[early:middle]:
+                multiply(n, h)
             if is_tile(nxt):
-                turn(nxt, "i", loaded[nxt]["i"])
+                if nxt == LAST:
+                    turn(nxt, "i", rows[nxt]["neg_u"], "neg_u")
+                else:
+                    turn(nxt, "i", loaded[nxt]["i"])
                 make_da_o(nxt)
             if is_tile(far):
                 if s < 0:
                     product_gho(far, nc.vector)
                 turn(far, "gho", rows[far]["gho"])
-            for n, h in todo[early:]:
+            for n, h in todo[middle:]:
                 multiply(n, h)
+            if s == BY_GATE[0]:
+                accs = {s: [psum_o.tile([P, N_TILE], F32, name="acc") for h in range(HALVES)]}
+                multiply_gate(s, GATE_O, accs[s], True, False)
             if is_tile(nxt):
                 make_neg_dc(nxt)
-            if is_tile(s) and s < NODE_TILES - 1:
+            if is_tile(s) and s != LAST:
                 make_da_u(s)
-            for c in range(CHUNKS):
-                if regroup_step(c) + 1 == s:
-                    quantise_chunk(c)
-            if is_tile(nxt):
-                quantise(nxt, GATE_O, GATE_I)
-            if is_tile(s) and s < NODE_TILES - 1:
-                quantise(s, GATE_I, GATES)
+            chunks = [c for c in range(CHUNKS) if regroup_step(c) + 1 == s]
+            for c in chunks:
+                quantise_chunk(c)
+            gates = ((s, GATE_I, GATES), (nxt, GATE_O, GATE_I)) if chunks else ((nxt, GATE_O, GATE_I), (s, GATE_I, GATES))
+            for n, first, after in gates:
+                if is_tile(n) and (n, first) != (LAST, GATE_I):
+                    quantise(n, first, after)
+            if far + 1 == LAST:
+                prepare_factors(far + 1)
             if s == 0:
                 product_iu(far + 1, nc.vector)
 
-        multiply_gate(NODE_TILES - 1, GATE_U, last_accs, False, False)
-        multiply_gate(NODE_TILES - 1, GATE_I, last_accs, False, True)
-        for h in range(HALVES):
-            store(NODE_TILES - 1, h, last_accs[h], h == HALVES - 1)
+        multiply_gate(LAST, GATE_I, accs[LAST], False, False)
+        multiply_gate(LAST, GATE_U, accs[LAST], False, True)
+        for part in range(LAST_PARTS):
+            store_part(LAST, 0, accs[LAST][0], part, nc.scalar.copy)
+            store_part(LAST, 1, accs[LAST][1], part, nc.vector.tensor_copy)

@@ -18,6 +18,7 @@ SIZE = 1024
 N_TILE = 512
 NODE_TILES = NODES // P
 LAST = NODE_TILES - 1
+FACTORED = (0, LAST)
 HALVES = SIZE // N_TILE
 GATES = 3
 GATE_O, GATE_I, GATE_U = 0, 1, 2
@@ -27,7 +28,7 @@ BYTES = NODES * CH * (2 + 3 * 4) + NODES * 2 * CH * 2 + GATES * CH * SIZE * 2 + 
 
 FIRST_STEP = -2
 CHUNKS = GATES * HALVES
-MULTIPLIES_PER_STEP = 4
+MULTIPLIES_PER_STEP = 3
 BY_GATE = (LAST - 1, LAST)
 LAST_PARTS = 2
 
@@ -198,27 +199,42 @@ def tile_treelstm_pb_v_kernel(
                 out=cols[n]["da"][:, GATE_U], in0=cols[n]["u_sq"][:], scalar=1.0, in1=cols[n]["q"][:], op0=ALU.subtract, op1=ALU.mult
             )
 
+        def square_u_rows(n):
+            u_sq = single.tile([P, CH], F32, name="u_sq_rows")
+            nc.scalar.activation(out=u_sq[:], in_=loaded[n]["u"][:], func=ACT.Square)
+            rows[n]["u_sq"] = u_sq
+
         def prepare_factors(n):
             i_1 = single.tile([P, CH], F32)
-            u_sq = single.tile([P, CH], F32, name="u_sq_rows")
             u_sq_1 = single.tile([P, CH], F32)
             nc.scalar.activation(out=i_1[:], in_=loaded[n]["i"][:], func=ACT.Identity, bias=-1.0)
-            nc.scalar.activation(out=u_sq[:], in_=loaded[n]["u"][:], func=ACT.Square)
-            nc.scalar.activation(out=u_sq_1[:], in_=u_sq[:], func=ACT.Identity, bias=-1.0)
+            square_u_rows(n)
+            nc.scalar.activation(out=u_sq_1[:], in_=rows[n]["u_sq"][:], func=ACT.Identity, bias=-1.0)
             rows[n]["i_1"] = i_1
             rows[n]["u_sq_1"] = u_sq_1
 
         def factor_i(n):
             neg_i = single.tile([P, CH], F32)
-            nc.gpsimd.tensor_tensor(out=neg_i[:], in0=rows[n]["i_1"][:], in1=rows[n]["iu"][:], op=ALU.mult)
-            rows[n]["neg_i"] = neg_i
+            if n == LAST:
+                nc.gpsimd.tensor_tensor(out=neg_i[:], in0=rows[n]["i_1"][:], in1=rows[n]["iu"][:], op=ALU.mult)
+            else:
+                nc.vector.scalar_tensor_tensor(
+                    out=neg_i[:], in0=loaded[n]["i"][:], scalar=1.0, in1=rows[n]["iu"][:], op0=ALU.subtract, op1=ALU.mult
+                )
+            rows[n]["neg_i"] = neg_i[:]
 
         def factor_u(n):
-            neg_u = mixed.tile([P, GATES * P * PACK // 2], F32, offset=0, align_bytes=64, name="gho")
-            nc.gpsimd.tensor_tensor(out=neg_u[:, 0:CH], in0=rows[n]["u_sq_1"][:], in1=loaded[n]["i"][:], op=ALU.mult)
-            rows[n]["neg_u"] = neg_u
+            if n == LAST:
+                neg_u = mixed.tile([P, GATES * P * PACK // 2], F32, offset=0, align_bytes=64, name="gho")
+                nc.gpsimd.tensor_tensor(out=neg_u[:, 0:CH], in0=rows[n]["u_sq_1"][:], in1=loaded[n]["i"][:], op=ALU.mult)
+            else:
+                neg_u = single.tile([P, CH], F32)
+                nc.vector.scalar_tensor_tensor(
+                    out=neg_u[:], in0=rows[n]["u_sq"][:], scalar=1.0, in1=loaded[n]["i"][:], op0=ALU.subtract, op1=ALU.mult
+                )
+            rows[n]["neg_u"] = neg_u[:, 0:CH]
 
-        def make_last_da(n, gate, factor):
+        def make_factored_da(n, gate, factor):
             nc.vector.tensor_tensor(out=cols[n]["da"][:, gate], in0=cols[n]["neg_dc"][:], in1=by_node(n, factor), op=ALU.mult)
 
         def quantise(n, first, after):
@@ -278,12 +294,10 @@ def tile_treelstm_pb_v_kernel(
 
         steps = range(FIRST_STEP, NODE_TILES)
 
-        for s in steps:
-            if is_tile(s - FIRST_STEP):
-                load_nodes(s - FIRST_STEP)
-            for c in range(CHUNKS):
-                if regroup_step(c) == s:
-                    load_chunk(c)
+        for n in range(NODE_TILES):
+            load_nodes(n)
+            if n < CHUNKS:
+                load_chunk(n)
 
         multiplied = [0] * HALVES
         for s in steps:
@@ -297,10 +311,12 @@ def tile_treelstm_pb_v_kernel(
                     multiplied[h] = upto
             early = (len(todo) + 1) // 2
             middle = early + (len(todo) - early) // 2
-            if s >= 0:
+            if s > 0:
                 regroup_chunks(s, CHUNKS - 1)
             if s == FIRST_STEP:
+                square_u_rows(far)
                 start_tile(far)
+                factor_u(far)
                 turn(far, "o", loaded[far]["o"])
             if is_tile(nxt):
                 turn_gc(nxt)
@@ -323,16 +339,18 @@ def tile_treelstm_pb_v_kernel(
                 factor_i(far)
             if nxt == LAST:
                 factor_u(nxt)
-            if is_tile(s) and s != LAST:
+            if is_tile(s) and s not in FACTORED:
                 make_q(s)
             if is_tile(nxt):
                 make_x(nxt)
             if is_tile(far) and s >= 0:
                 turn(far, "o", loaded[far]["o"])
-            if is_tile(s) and s != LAST:
+            if s in FACTORED:
+                make_factored_da(s, GATE_I, "neg_i")
+            elif is_tile(s):
                 make_w(s)
             if is_tile(nxt):
-                if nxt == LAST:
+                if nxt in FACTORED:
                     turn(nxt, "u", rows[nxt]["neg_i"], "neg_i")
                 else:
                     turn(nxt, "u", loaded[nxt]["u"])
@@ -343,21 +361,21 @@ def tile_treelstm_pb_v_kernel(
                 turn(far, "o", loaded[far]["o"])
             if s >= -1 and is_tile(far + 1) and s != 0:
                 product_iu(far + 1, nc.gpsimd)
-            if s < 0:
+            if s <= 0:
                 regroup_chunks(s, CHUNKS - 1)
             if s == regroup_step(CHUNKS - 1):
                 regroup_chunk(CHUNKS - 1)
-            if is_tile(s) and s != LAST:
+            if s in FACTORED:
+                make_factored_da(s, GATE_U, "neg_u")
+            elif is_tile(s):
                 make_da_i(s)
             if s == LAST:
-                make_last_da(s, GATE_I, "neg_i")
-                make_last_da(s, GATE_U, "neg_u")
                 quantise(s, GATE_I, GATE_U)
                 quantise(s, GATE_U, GATES)
             for n, h in todo[early:middle]:
                 multiply(n, h)
             if is_tile(nxt):
-                if nxt == LAST:
+                if nxt in FACTORED:
                     turn(nxt, "i", rows[nxt]["neg_u"], "neg_u")
                 else:
                     turn(nxt, "i", loaded[nxt]["i"])
@@ -365,6 +383,8 @@ def tile_treelstm_pb_v_kernel(
             if is_tile(far):
                 if s < 0:
                     product_gho(far, nc.vector)
+                if far == FACTORED[0]:
+                    factor_i(far)
                 turn(far, "gho", rows[far]["gho"])
             for n, h in todo[middle:]:
                 multiply(n, h)
@@ -373,7 +393,7 @@ def tile_treelstm_pb_v_kernel(
                 multiply_gate(s, GATE_O, accs[s], True, False)
             if is_tile(nxt):
                 make_neg_dc(nxt)
-            if is_tile(s) and s != LAST:
+            if is_tile(s) and s not in FACTORED:
                 make_da_u(s)
             chunks = [c for c in range(CHUNKS) if regroup_step(c) + 1 == s]
             for c in chunks:

@@ -28,13 +28,13 @@ BYTES = NODES * CH * (2 + 3 * 4) + NODES * 2 * CH * 2 + GATES * CH * SIZE * 2 + 
 
 FIRST_STEP = -2
 CHUNKS = GATES * HALVES
-MULTIPLIES_PER_STEP = 3
+MULTIPLIES_PER_STEP = 4
 BY_GATE = (LAST - 1, LAST)
 LAST_PARTS = 2
 
 
 def regroup_step(c):
-    return min(c, CHUNKS - 2) + FIRST_STEP
+    return min(c, CHUNKS - 2) + FIRST_STEP + 1
 
 
 def tile_treelstm_pb_v_kernel(
@@ -109,7 +109,7 @@ def tile_treelstm_pb_v_kernel(
             )
 
         def product_iu(n, engine):
-            iu = single.tile([P, CH], F32)
+            iu = work.tile([P, CH], F32)
             engine.tensor_tensor(out=iu[:], in0=loaded[n]["i"][:], in1=loaded[n]["u"][:], op=ALU.mult)
             rows[n]["iu"] = iu
 
@@ -296,8 +296,8 @@ def tile_treelstm_pb_v_kernel(
 
         for n in range(NODE_TILES):
             load_nodes(n)
-            if n < CHUNKS:
-                load_chunk(n)
+            if 0 < n <= CHUNKS:
+                load_chunk(n - 1)
 
         multiplied = [0] * HALVES
         for s in steps:

import concourse.mybir as mybir
from concourse.masks import make_identity

F32 = mybir.dt.float32
BF16 = mybir.dt.bfloat16
U32 = mybir.dt.uint32
U8 = mybir.dt.uint8
E4M3_X4 = mybir.dt.float8_e4m3fn_x4
E5M2_X4 = mybir.dt.float8_e5m2_x4
ALU = mybir.AluOpType
ACT = mybir.ActivationFunctionType

P = 128
PACK = 4
NODES = 1024
CH = 512
SIZE = 1024
N_TILE = 512
NODE_TILES = NODES // P
LAST = NODE_TILES - 1
FACTORED = (0, LAST)
HALVES = SIZE // N_TILE
GATES = 3
GATE_O, GATE_I, GATE_U = 0, 1, 2

FLOPS = 2 * NODES * SIZE * CH * GATES
BYTES = NODES * CH * (2 + 3 * 4) + NODES * 2 * CH * 2 + GATES * CH * SIZE * 2 + NODES * SIZE * 4

FIRST_STEP = -2
CHUNKS = GATES * HALVES
MULTIPLIES_PER_STEP = 4
BY_GATE = (LAST - 1, LAST)
LAST_PARTS = 2


def regroup_step(c):
    return min(c, CHUNKS - 2) + FIRST_STEP + 1


def tile_treelstm_pb_v_kernel(
    tc, z0, h_tilde, fc_sum, W_i, U_i, b_i, W_o, U_o, b_o, W_u, U_u, b_u, i_j, o_j, u_j, grad_out, out
):
    nc = tc.nc
    weights = (W_o, W_i, W_u)

    with tc.tile_pool(name="const", bufs=1) as const, tc.tile_pool(name="inputs", bufs=NODE_TILES) as inputs, tc.tile_pool(
        name="wraw", bufs=CHUNKS
    ) as wraw, tc.tile_pool(name="wgrp", bufs=3) as wgrp, tc.tile_pool(name="mixed", bufs=3) as mixed, tc.tile_pool(
        name="work", bufs=2
    ) as work, tc.tile_pool(name="single", bufs=1) as single, tc.tile_pool(name="ahead", bufs=3) as ahead, tc.tile_pool(name="codes", bufs=NODE_TILES) as codes, tc.tile_pool(
        name="results", bufs=6
    ) as results, tc.psum_pool(name="psum_t", bufs=1) as psum_t, tc.psum_pool(name="psum_o", bufs=2) as psum_o, tc.manual_schedule():
        ident = const.tile([P, P], BF16)
        make_identity(nc, ident[:])
        ident_f32 = const.tile([P, P], F32)
        make_identity(nc, ident_f32[:])
        w_codes = const.tile([P, CHUNKS, N_TILE], U32, align_bytes=64)
        w_scales = const.tile([P, CHUNKS, N_TILE], U8, align_bytes=64)

        loaded = {}
        w_raw = {}
        w_grouped = {}
        rows = {}
        turned = {}
        cols = {}
        da_packed = {}

        def load_nodes(n):
            r = slice(n * P, (n + 1) * P)
            i_sb = inputs.tile([P, CH], F32)
            u_sb = inputs.tile([P, CH], F32)
            g_sb = inputs.tile([P, 2 * CH], BF16)
            o_sb = inputs.tile([P, CH], F32)
            fc_sb = inputs.tile([P, CH], BF16)
            nc.sync.dma_start(out=i_sb[:], in_=i_j[r, :])
            nc.sync.dma_start(out=u_sb[:], in_=u_j[r, :])
            nc.sync.dma_start(out=fc_sb[:], in_=fc_sum[r, :])
            nc.sync.dma_start(out=g_sb[:], in_=grad_out[r, :])
            nc.sync.dma_start(out=o_sb[:], in_=o_j[r, :])
            loaded[n] = {"i": i_sb, "o": o_sb, "u": u_sb, "fc": fc_sb, "g": g_sb}
            rows[n] = {}
            turned[n] = {}
            cols[n] = {}

        def load_chunk(c):
            h, g = divmod(c, GATES)
            raw = wraw.tile([P, PACK, N_TILE], BF16)
            nc.sync.dma_start(out=raw[:], in_=weights[g][:, h * N_TILE : (h + 1) * N_TILE].rearrange("(t p) n -> p t n", p=P))
            w_raw[c] = raw

        def regroup_chunk(c):
            w_grp = wgrp.tile([P, N_TILE, PACK], BF16, align_bytes=64)
            nc.scalar.copy(
                out=w_grp[:].rearrange("p (c i) t -> p c t i", i=4),
                in_=w_raw[c][:].rearrange("p t (c i) -> p c t i", i=4),
            )
            w_grouped[c] = w_grp

        def regroup_chunks(s, upto):
            for c in range(upto):
                if regroup_step(c) == s:
                    regroup_chunk(c)

        def quantise_chunk(c):
            nc.vector.quantize_mx(
                out=w_codes[:, c, :].bitcast(E4M3_X4),
                scales=w_scales[:, c, :],
                in_=w_grouped[c][:].rearrange("p n t -> p (n t)"),
            )

        def product_iu(n, engine):
            iu = work.tile([P, CH], F32)
            engine.tensor_tensor(out=iu[:], in0=loaded[n]["i"][:], in1=loaded[n]["u"][:], op=ALU.mult)
            rows[n]["iu"] = iu

        def product_gho(n, engine):
            gho = mixed.tile([P, GATES * P * PACK // 2], F32, offset=0, align_bytes=64, name="gho")
            engine.tensor_tensor(out=gho[:, 0:CH], in0=loaded[n]["g"][:, 0:CH], in1=loaded[n]["o"][:], op=ALU.mult)
            rows[n]["gho"] = gho

        def block(t):
            return slice(t * P, (t + 1) * P)

        def turn_fc(n):
            cell_t = psum_t.tile([P, PACK, P], F32)
            for t in range(PACK):
                nc.tensor.matmul(out=cell_t[:, t, :], lhsT=loaded[n]["fc"][:, block(t)], rhs=ident[:], start=(t == 0), stop=False)
            turned[n]["cell"] = cell_t

        def turn_cell(n):
            for t in range(PACK):
                nc.tensor.matmul(
                    out=turned[n]["cell"][:, t, :],
                    lhsT=rows[n]["iu"][:, block(t)],
                    rhs=ident_f32[:],
                    is_transpose=True,
                    start=False,
                    stop=(t == PACK - 1),
                )

        def turn(n, bank, source, what=None):
            turned_tile = psum_t.tile([P, PACK, P], F32, name=bank + "_t")
            for t in range(PACK):
                nc.tensor.transpose(turned_tile[:, t, :], source[:, block(t)], ident_f32[:])
            turned[n][what or bank] = turned_tile

        def turn_gc(n):
            gc_t = psum_t.tile([P, PACK, P], F32)
            for t in range(PACK):
                gc = loaded[n]["g"][:, CH + t * P : CH + (t + 1) * P]
                nc.tensor.matmul(out=gc_t[:, t, :], lhsT=gc, rhs=ident[:], start=(t == 0), stop=(t == PACK - 1))
            turned[n]["gc"] = gc_t

        def by_node(n, what):
            return turned[n][what][:].rearrange("p t n -> p n t")

        def new_cols(n, what, pool):
            tile = pool.tile([P, P, PACK], F32, name=what)
            cols[n][what] = tile
            return tile[:]

        def tanh(n):
            nc.scalar.activation(out=new_cols(n, "neg_tc", ahead), in_=by_node(n, "cell"), func=ACT.Tanh, scale=-1.0)
            nc.scalar.activation(out=new_cols(n, "tc_sq", ahead), in_=cols[n]["neg_tc"][:], func=ACT.Square)

        def square_u(n):
            nc.scalar.activation(out=new_cols(n, "u_sq", work), in_=by_node(n, "u"), func=ACT.Square)

        def make_x(n):
            nc.vector.scalar_tensor_tensor(
                out=new_cols(n, "x", work), in0=by_node(n, "o"), scalar=1.0, in1=cols[n]["neg_tc"][:], op0=ALU.subtract, op1=ALU.mult
            )

        def make_masked(n):
            nc.vector.scalar_tensor_tensor(
                out=new_cols(n, "masked", work), in0=cols[n]["tc_sq"][:], scalar=1.0, in1=by_node(n, "gho"), op0=ALU.subtract, op1=ALU.mult
            )

        def make_da_o(n):
            cols[n]["da"] = mixed.tile([P, GATES, P, PACK], BF16, offset=0, align_bytes=64, name="da")
            nc.vector.tensor_tensor(out=cols[n]["da"][:, GATE_O], in0=cols[n]["x"][:], in1=by_node(n, "gho"), op=ALU.mult)

        def make_neg_dc(n):
            nc.vector.tensor_tensor(out=new_cols(n, "neg_dc", work), in0=cols[n]["masked"][:], in1=by_node(n, "gc"), op=ALU.subtract)

        def make_q(n):
            nc.vector.tensor_tensor(out=new_cols(n, "q", work), in0=cols[n]["neg_dc"][:], in1=by_node(n, "i"), op=ALU.mult)

        def make_w(n):
            nc.vector.tensor_tensor(out=new_cols(n, "w", work), in0=cols[n]["q"][:], in1=by_node(n, "u"), op=ALU.mult)

        def make_da_i(n):
            nc.vector.scalar_tensor_tensor(
                out=cols[n]["da"][:, GATE_I], in0=by_node(n, "i"), scalar=1.0, in1=cols[n]["w"][:], op0=ALU.subtract, op1=ALU.mult
            )

        def make_da_u(n):
            nc.vector.scalar_tensor_tensor(
                out=cols[n]["da"][:, GATE_U], in0=cols[n]["u_sq"][:], scalar=1.0, in1=cols[n]["q"][:], op0=ALU.subtract, op1=ALU.mult
            )

        def square_u_rows(n):
            u_sq = single.tile([P, CH], F32, name="u_sq_rows")
            nc.scalar.activation(out=u_sq[:], in_=loaded[n]["u"][:], func=ACT.Square)
            rows[n]["u_sq"] = u_sq

        def prepare_factors(n):
            i_1 = single.tile([P, CH], F32)
            u_sq_1 = single.tile([P, CH], F32)
            nc.scalar.activation(out=i_1[:], in_=loaded[n]["i"][:], func=ACT.Identity, bias=-1.0)
            square_u_rows(n)
            nc.scalar.activation(out=u_sq_1[:], in_=rows[n]["u_sq"][:], func=ACT.Identity, bias=-1.0)
            rows[n]["i_1"] = i_1
            rows[n]["u_sq_1"] = u_sq_1

        def factor_i(n):
            neg_i = single.tile([P, CH], F32)
            if n == LAST:
                nc.gpsimd.tensor_tensor(out=neg_i[:], in0=rows[n]["i_1"][:], in1=rows[n]["iu"][:], op=ALU.mult)
            else:
                nc.vector.scalar_tensor_tensor(
                    out=neg_i[:], in0=loaded[n]["i"][:], scalar=1.0, in1=rows[n]["iu"][:], op0=ALU.subtract, op1=ALU.mult
                )
            rows[n]["neg_i"] = neg_i[:]

        def factor_u(n):
            if n == LAST:
                neg_u = mixed.tile([P, GATES * P * PACK // 2], F32, offset=0, align_bytes=64, name="gho")
                nc.gpsimd.tensor_tensor(out=neg_u[:, 0:CH], in0=rows[n]["u_sq_1"][:], in1=loaded[n]["i"][:], op=ALU.mult)
            else:
                neg_u = single.tile([P, CH], F32)
                nc.vector.scalar_tensor_tensor(
                    out=neg_u[:], in0=rows[n]["u_sq"][:], scalar=1.0, in1=loaded[n]["i"][:], op0=ALU.subtract, op1=ALU.mult
                )
            rows[n]["neg_u"] = neg_u[:, 0:CH]

        def make_factored_da(n, gate, factor):
            nc.vector.tensor_tensor(out=cols[n]["da"][:, gate], in0=cols[n]["neg_dc"][:], in1=by_node(n, factor), op=ALU.mult)

        def quantise(n, first, after):
            if n not in da_packed:
                da_codes = codes.tile([P, GATES, P], U32, align_bytes=64)
                da_scales = codes.tile([P, GATES, P], U8, align_bytes=64)
                da_packed[n] = (da_codes, da_scales)
            da_codes, da_scales = da_packed[n]
            nc.vector.quantize_mx(
                out=da_codes[:, first:after, :].rearrange("p g n -> p (g n)").bitcast(E5M2_X4),
                scales=da_scales[:, first:after, :].rearrange("p g n -> p (g n)"),
                in_=cols[n]["da"][:, first:after].rearrange("p g n t -> p (g n t)"),
            )

        def one_pass(n, h, g, acc, first, last):
            da_codes, da_scales = da_packed[n]
            nc.tensor.matmul_mx(
                out=acc[:],
                lhsT=da_codes[:, g, :].bitcast(E5M2_X4),
                lhsT_scale=da_scales[:, g, :],
                rhs=w_codes[:, h * GATES + g, :].bitcast(E4M3_X4),
                rhs_scale=w_scales[:, h * GATES + g, :],
                start=first,
                stop=last,
            )

        def store(n, h, acc):
            result = results.tile([P, N_TILE], F32)
            nc.scalar.copy(out=result[:], in_=acc[:])
            nc.sync.dma_start(out=out[n * P : (n + 1) * P, h * N_TILE : (h + 1) * N_TILE], in_=result[:])

        def store_part(n, h, acc, part, copy):
            width = N_TILE // LAST_PARTS
            result = single.tile([P, width], F32, name="last_%d_%d" % (h, part))
            copy(out=result[:], in_=acc[:, part * width : (part + 1) * width])
            first = h * N_TILE + part * width
            nc.sync.dma_start(out=out[n * P : (n + 1) * P, first : first + width], in_=result[:])

        def multiply(n, h):
            acc = psum_o.tile([P, N_TILE], F32)
            for g in range(GATES):
                one_pass(n, h, g, acc, g == 0, g == GATES - 1)
            store(n, h, acc)

        def multiply_gate(n, g, accs, first, last):
            for h in range(HALVES):
                one_pass(n, h, g, accs[h], first, last)

        def start_tile(n):
            product_iu(n, nc.vector)
            turn_fc(n)
            turn_cell(n)
            tanh(n)

        def is_tile(n):
            return 0 <= n < NODE_TILES

        steps = range(FIRST_STEP, NODE_TILES)

        for n in range(NODE_TILES):
            load_nodes(n)
            if 0 < n <= CHUNKS:
                load_chunk(n - 1)

        multiplied = [0] * HALVES
        for s in steps:
            nxt = s + 1
            far = s + 2
            todo = []
            for h in range(HALVES):
                if s >= regroup_step((h + 1) * GATES - 1) + 2:
                    upto = min(s, BY_GATE[0], multiplied[h] + MULTIPLIES_PER_STEP - len(todo))
                    todo += [(n, h) for n in range(multiplied[h], upto)]
                    multiplied[h] = upto
            early = (len(todo) + 1) // 2
            middle = early + (len(todo) - early) // 2
            if s > 0:
                regroup_chunks(s, CHUNKS - 1)
            if s == FIRST_STEP:
                square_u_rows(far)
                start_tile(far)
                factor_u(far)
                turn(far, "o", loaded[far]["o"])
            if is_tile(nxt):
                turn_gc(nxt)
            if is_tile(far) and s >= 0:
                turn_fc(far)
            if s == LAST:
                accs[s] = [psum_t.tile([P, N_TILE], F32, name=what + "_t") for what in ("cell", "o")]
                multiply_gate(s, GATE_O, accs[s], True, False)
                multiply_gate(s - 1, GATE_I, accs[s - 1], False, False)
                multiply_gate(s - 1, GATE_U, accs[s - 1], False, True)
                for h in range(HALVES):
                    store(s - 1, h, accs[s - 1][h])
            for n, h in todo[:early]:
                multiply(n, h)
            if is_tile(far) and s >= 0:
                turn_cell(far)
                tanh(far)
                product_gho(far, nc.gpsimd)
            if far == LAST:
                factor_i(far)
            if nxt == LAST:
                factor_u(nxt)
            if is_tile(s) and s not in FACTORED:
                make_q(s)
            if is_tile(nxt):
                make_x(nxt)
            if is_tile(far) and s >= 0:
                turn(far, "o", loaded[far]["o"])
            if s in FACTORED:
                make_factored_da(s, GATE_I, "neg_i")
            elif is_tile(s):
                make_w(s)
            if is_tile(nxt):
                if nxt in FACTORED:
                    turn(nxt, "u", rows[nxt]["neg_i"], "neg_i")
                else:
                    turn(nxt, "u", loaded[nxt]["u"])
                    square_u(nxt)
                make_masked(nxt)
            if is_tile(far) and FIRST_STEP < s < 0:
                start_tile(far)
                turn(far, "o", loaded[far]["o"])
            if s >= -1 and is_tile(far + 1) and s != 0:
                product_iu(far + 1, nc.gpsimd)
            if s <= 0:
                regroup_chunks(s, CHUNKS - 1)
            if s == regroup_step(CHUNKS - 1):
                regroup_chunk(CHUNKS - 1)
            if s in FACTORED:
                make_factored_da(s, GATE_U, "neg_u")
            elif is_tile(s):
                make_da_i(s)
            if s == LAST:
                quantise(s, GATE_I, GATE_U)
                quantise(s, GATE_U, GATES)
            for n, h in todo[early:middle]:
                multiply(n, h)
            if is_tile(nxt):
                if nxt in FACTORED:
                    turn(nxt, "i", rows[nxt]["neg_u"], "neg_u")
                else:
                    turn(nxt, "i", loaded[nxt]["i"])
                make_da_o(nxt)
            if is_tile(far):
                if s < 0:
                    product_gho(far, nc.vector)
                if far == FACTORED[0]:
                    factor_i(far)
                turn(far, "gho", rows[far]["gho"])
            for n, h in todo[middle:]:
                multiply(n, h)
            if s == BY_GATE[0]:
                accs = {s: [psum_o.tile([P, N_TILE], F32, name="acc") for h in range(HALVES)]}
                multiply_gate(s, GATE_O, accs[s], True, False)
            if is_tile(nxt):
                make_neg_dc(nxt)
            if is_tile(s) and s not in FACTORED:
                make_da_u(s)
            chunks = [c for c in range(CHUNKS) if regroup_step(c) + 1 == s]
            for c in chunks:
                quantise_chunk(c)
            gates = ((s, GATE_I, GATES), (nxt, GATE_O, GATE_I)) if chunks else ((nxt, GATE_O, GATE_I), (s, GATE_I, GATES))
            for n, first, after in gates:
                if is_tile(n) and (n, first) != (LAST, GATE_I):
                    quantise(n, first, after)
            if far + 1 == LAST:
                prepare_factors(far + 1)
            if s == 0:
                product_iu(far + 1, nc.vector)

        multiply_gate(LAST, GATE_I, accs[LAST], False, False)
        multiply_gate(LAST, GATE_U, accs[LAST], False, True)
        for part in range(LAST_PARTS):
            store_part(LAST, 0, accs[LAST][0], part, nc.scalar.copy)
            store_part(LAST, 1, accs[LAST][1], part, nc.vector.tensor_copy)
